import numpy as np
import ml_dtypes


def mxq(x, axis, fmt="e4m3"):
    dtype, down = {"e4m3": (ml_dtypes.float8_e4m3fn, 7), "e5m2": (ml_dtypes.float8_e5m2, 14)}[fmt]
    v = np.moveaxis(np.asarray(x, np.float32).astype(ml_dtypes.bfloat16).astype(np.float64), axis, -1)
    blocks = v.reshape(v.shape[:-1] + (-1, 32))
    amax = np.abs(blocks).max(-1, keepdims=True)
    byte = np.maximum(np.where(amax > 0, np.frexp(amax)[1] - 1 + 127, 0) - down, 1)
    scale = np.exp2(byte - 127.0)
    codes = (blocks / scale).astype(np.float32).astype(dtype).astype(np.float64)
    return np.moveaxis((codes * scale).reshape(v.shape), -1, axis)


WIDE = False


def mx_kscale(k):
    if not WIDE:
        return np.ones(k)
    levels = np.array([10, -10, 5, -5, 0])
    a = np.random.permutation(np.resize(levels, k // 512 * 4)).reshape(k // 512, 4)
    idx = np.arange(k)
    return np.exp2(a[idx // 512, idx % 128 // 32])


BF16 = ml_dtypes.bfloat16


def bf(x):
    return np.asarray(x, np.float32).astype(BF16)


def f64(x):
    return np.asarray(x).astype(np.float64)


B, T, N, M, A, C, Q, D = 2, 2, 128, 128, 12288, 4096, 512, 512
G = A + C
DILATION = 1.5
MIN_EXTENT = 0.5
GATE_TEMP = 3.0
FEAT_TEMP = 6.0
KEEP_W = 0.5


def l2norm(x, eps=1e-12):
    n = np.sqrt((x * x).sum(axis=-1, keepdims=True))
    return x / np.maximum(n, eps)


def setup_inputs():
    s, u = mx_kscale(G), mx_kscale(Q)
    return {
        "center": bf(np.random.standard_normal((B, T, N * 3)) * 5.0),
        "instance_affinity": bf(np.random.standard_normal((B, T, N, A)) * s[:A]),
        "motion_code": bf(np.random.standard_normal((B, T, N, C)) * s[A:]),
        "keep_score": bf(np.maximum(np.random.uniform(-0.05, 0.99, (B, T, N)), 0.0)),
        "query_box3d": bf(np.random.standard_normal((B, T, M, 7)) * 3.0),
        "query_feat": bf(np.random.standard_normal((B, T, M, Q)) * u),
        "presence_logit": bf(np.random.standard_normal((B, T, M))),
        "Wq": bf(np.random.standard_normal((D, Q)) / np.sqrt(Q) / u),
        "bq": bf(np.random.standard_normal(D) * 0.5),
        "Wg": bf(np.random.standard_normal((D, G)) / np.sqrt(G) / s),
        "bg": bf(np.random.standard_normal(D) * 0.5),
        "background_bias": bf(0.5 + 0.1 * np.random.standard_normal(1)),
    }


def reference(center, instance_affinity, motion_code, keep_score, query_box3d,
              query_feat, presence_logit, Wq, bq, Wg, bg, background_bias):
    b, t = center.shape[:2]
    centers = f64(center).reshape(b, t, -1, 3)
    qbox = f64(query_box3d)[..., :7]
    q_centers = qbox[..., :3]
    q_sizes = np.maximum(np.abs(qbox[..., 3:6]), MIN_EXTENT)

    delta = np.abs(centers[:, :, :, None, :] - q_centers[:, :, None, :, :])
    normalized = delta / (0.5 * DILATION * q_sizes[:, :, None, :, :])
    signed_distance = normalized.max(axis=-1) - 1.0
    gate_logit = np.clip(-signed_distance * GATE_TEMP, -8.0, 8.0)

    gfeat = np.concatenate([f64(instance_affinity), f64(motion_code)], axis=-1)
    gfeat = gfeat.reshape(b, t, -1, gfeat.shape[-1])
    qf = l2norm((mxq(f64(query_feat), 3, "e4m3") @ mxq(f64(Wq), 1, "e4m3").T) + f64(bq))
    gf = l2norm((mxq(gfeat, 3, "e4m3") @ mxq(f64(Wg), 1, "e4m3").T) + f64(bg))
    feature_similarity = mxq(gf, 3, "e4m3") @ mxq(qf, 3, "e4m3").transpose(0, 1, 3, 2)

    presence = f64(presence_logit)[:, :, None, :]
    ks = np.clip(f64(keep_score).reshape(b, t, -1, 1), 1e-4, 1.0 - 1e-4)
    routing_keep = np.log(ks) - np.log1p(-ks)

    fg_logits = presence + FEAT_TEMP * feature_similarity + gate_logit + KEEP_W * routing_keep
    bg_logits = np.zeros_like(fg_logits[..., :1]) + f64(background_bias)
    logits = np.concatenate([bg_logits, fg_logits], axis=-1)
    e = np.exp(logits - logits.max(axis=-1, keepdims=True))
    probs = e / e.sum(axis=-1, keepdims=True)
    return probs.reshape(b, -1, probs.shape[-1])

@@ -1,0 +1,415 @@
+from contextlib import ExitStack
+
+import concourse.mybir as mybir
+from concourse.masks import make_identity
+
+F32 = mybir.dt.float32
+BF16 = mybir.dt.bfloat16
+U32 = mybir.dt.uint32
+U8 = mybir.dt.uint8
+FP8X4 = mybir.dt.float8_e4m3fn_x4
+ALU = mybir.AluOpType
+ACT = mybir.ActivationFunctionType
+AXIS = mybir.AxisListType
+
+P = 128
+PACK = 4
+K_PASS = P * PACK
+PASS_WORDS = K_PASS // 2
+PAIRS = 4
+FEATURES = 512
+AFFINITY = 12288
+MOTION = 4096
+CHUNK_PASSES = 4
+CHUNK = CHUNK_PASSES * K_PASS
+CHUNKS = (AFFINITY + MOTION) // CHUNK
+ROUND_BANKS = 4
+SCALAR_BANKS = 3
+BANK_VALUES = 2 * P * PACK
+RAW_BUFS = 8
+POSITIONS = PAIRS * P * 3
+SPREAD = POSITIONS + 2 * FEATURES
+
+DILATION = 1.5
+MIN_EXTENT = 0.5
+GATE_TEMP = 3.0
+GATE_CLIP = 8.0
+FEAT_TEMP = 6.0
+KEEP_W = 0.5
+KEEP_EPS = 1e-4
+NORM_EPS = 1e-12
+
+FLOPS = 2 * PAIRS * P * FEATURES * (AFFINITY + MOTION + K_PASS) + 2 * PAIRS * P * P * FEATURES
+
+
+def tile_gaussianqueryassignment_k_kernel(
+    tc,
+    center,
+    instance_affinity,
+    motion_code,
+    keep_score,
+    query_box3d,
+    query_feat,
+    presence_logit,
+    Wq,
+    bq,
+    Wg,
+    bg,
+    background_bias,
+    out,
+):
+    nc = tc.nc
+    with ExitStack() as ctx:
+        ctx.enter_context(tc.manual_schedule())
+        consts = ctx.enter_context(tc.tile_pool(name="consts", bufs=1))
+        raws = ctx.enter_context(tc.tile_pool(name="raws", bufs=RAW_BUFS))
+        groupeds = ctx.enter_context(tc.tile_pool(name="groupeds", bufs=3))
+        operands = ctx.enter_context(tc.tile_pool(name="operands", bufs=2))
+        per_pair = ctx.enter_context(tc.tile_pool(name="per_pair", bufs=PAIRS))
+        flip_psum = ctx.enter_context(tc.psum_pool(name="flip_psum", bufs=ROUND_BANKS))
+        acc_psum = ctx.enter_context(tc.psum_pool(name="acc_psum", bufs=1))
+
+        ident_f32 = consts.tile([P, P], F32, name="ident_f32")
+        make_identity(nc, ident_f32[:])
+        ident_bf16 = consts.tile([P, P], BF16, name="ident_bf16")
+        make_identity(nc, ident_bf16[:])
+        ones = consts.tile([P, P], BF16, name="ones")
+        nc.vector.memset(ones[:], 1.0)
+
+        row0 = consts.tile([P, SPREAD], BF16, name="row0")
+        nc.vector.memset(row0[:], 0.0)
+        nc.scalar.dma_start(out=row0[0:1, 0:POSITIONS], in_=center.rearrange("(o b) t x -> o (b t x)", o=1))
+        nc.scalar.dma_start(
+            out=row0[0:1, POSITIONS : POSITIONS + FEATURES], in_=bq.rearrange("(o d) -> o d", o=1)
+        )
+        nc.scalar.dma_start(out=row0[0:1, POSITIONS + FEATURES : SPREAD], in_=bg.rearrange("(o d) -> o d", o=1))
+
+        box = consts.tile([P, PAIRS, 7], BF16, name="box")
+        nc.gpsimd.dma_start(out=box[:], in_=query_box3d.rearrange("b t m f -> m (b t) f"))
+        keep = consts.tile([P, PAIRS], BF16, name="keep")
+        presence = consts.tile([P, PAIRS], BF16, name="presence")
+        with nc.allow_non_contiguous_dma(reason="512 single values, one to a partition and pair"):
+            nc.gpsimd.dma_start(out=keep[:], in_=keep_score.rearrange("b t n -> n (b t)"))
+            nc.gpsimd.dma_start(out=presence[:], in_=presence_logit.rearrange("b t m -> m (b t)"))
+        background = consts.tile([P, 1], BF16, name="background")
+        nc.gpsimd.dma_start(out=background[:], in_=background_bias.partition_broadcast(P))
+
+        def flip_round(sources):
+            banks = []
+            for source in sources:
+                bank = flip_psum.tile([P, 2, 2, P], F32, name="bank", tag="bank")
+                for block in range(2):
+                    for half in range(2):
+                        nc.tensor.transpose(
+                            bank[:, block, half, :], source[:, block, half * P : (half + 1) * P], ident_f32[:]
+                        )
+                banks.append(bank)
+            return banks
+
+        def empty_round(banks):
+            grouped = groupeds.tile([P, ROUND_BANKS * BANK_VALUES], BF16, name="grouped", tag="grouped", align_bytes=64)
+            words = grouped[:].bitcast(F32).rearrange("p (i b r h) -> p i b r h", i=ROUND_BANKS, b=2, h=2)
+            for i, bank in enumerate(banks):
+                flipped = bank[:].rearrange("p b h r -> p b r h")
+                if i < SCALAR_BANKS:
+                    nc.scalar.copy(out=words[:, i], in_=flipped)
+                else:
+                    nc.vector.tensor_copy(out=words[:, i], in_=flipped)
+            return grouped
+
+        def quantise_round(grouped, codes_parts, scales_parts):
+            for i in range(ROUND_BANKS):
+                nc.vector.quantize_mx(
+                    out=codes_parts[i].bitcast(FP8X4),
+                    scales=scales_parts[i],
+                    in_=grouped[:, i * BANK_VALUES : (i + 1) * BANK_VALUES],
+                )
+
+        def operand_tiles(passes):
+            codes = operands.tile([P, passes, 2, PAIRS * P], U32, name="codes", tag="codes%d" % passes, align_bytes=64)
+            scales = operands.tile([P, passes, 2, PAIRS * P], U8, name="scales", tag="scales%d" % passes, align_bytes=64)
+            return codes, scales
+
+        def project(codes, scales, k_pass, pair, acc, start, stop):
+            rows = slice(pair * P, (pair + 1) * P)
+            nc.tensor.matmul_mx(
+                out=acc[:],
+                lhsT=codes[:, k_pass, 0, rows].bitcast(FP8X4),
+                lhsT_scale=scales[:, k_pass, 0, rows],
+                rhs=codes[:, k_pass, 1, :].bitcast(FP8X4),
+                rhs_scale=scales[:, k_pass, 1, :],
+                start=start,
+                stop=stop,
+            )
+
+        def accumulators():
+            return [acc_psum.tile([P, FEATURES], F32, name="acc%d" % pair, tag="acc%d" % pair) for pair in range(PAIRS)]
+
+        def run_tick(stages, tick):
+            for s, stage in enumerate(stages):
+                pair = tick - s
+                if 0 <= pair < PAIRS:
+                    stage(pair)
+
+        def ticks(stages):
+            return PAIRS + len(stages) - 1
+
+        def unit_row_stages(acc, bias, unit_codes, unit_scales):
+            held = {}
+
+            def add_bias_and_square(pair):
+                biased = per_pair.tile([P, FEATURES], F32, name="biased", tag="biased")
+                nc.vector.tensor_tensor(out=biased[:], in0=acc[pair][:], in1=bias, op=ALU.add)
+                squares = per_pair.tile([P, FEATURES], F32, name="squares", tag="squares")
+                sum_squares = per_pair.tile([P, 1], F32, name="sum_squares", tag="sum_squares")
+                nc.scalar.activation(out=squares[:], in_=biased[:], func=ACT.Square, accum_out=sum_squares[:])
+                held["biased", pair] = biased
+                held["sum_squares", pair] = sum_squares
+
+            def take_norm(pair):
+                floored = per_pair.tile([P, 1], F32, name="floored", tag="floored")
+                nc.vector.tensor_scalar_max(out=floored[:], in0=held["sum_squares", pair][:], scalar1=NORM_EPS * NORM_EPS)
+                norm = per_pair.tile([P, 1], F32, name="norm", tag="norm")
+                nc.scalar.sqrt(out=norm[:], in_=floored[:])
+                held["norm", pair] = norm
+
+            def scale_rows(pair):
+                inv_norm = per_pair.tile([P, 1], F32, name="inv_norm", tag="inv_norm")
+                nc.vector.reciprocal(out=inv_norm[:], in_=held["norm", pair][:])
+                unit = per_pair.tile([P, FEATURES], BF16, name="unit", tag="unit")
+                nc.vector.tensor_scalar_mul(out=unit[:], in0=held["biased", pair][:], scalar1=inv_norm[:, 0:1])
+                held["unit", pair] = unit
+
+            def flip_rows(pair):
+                bank = flip_psum.tile([P, PACK, P], BF16, name="unit_bank", tag="bank")
+                for t in range(PACK):
+                    nc.tensor.transpose(bank[:, t, :], held["unit", pair][:, t * P : (t + 1) * P], ident_bf16[:])
+                grouped = per_pair.tile([P, P, PACK], BF16, name="unit_grouped", tag="unit_grouped", align_bytes=64)
+                nc.scalar.copy(out=grouped[:], in_=bank[:].rearrange("p t r -> p r t"))
+                held["grouped", pair] = grouped
+
+            def quantise_rows(pair):
+                nc.vector.quantize_mx(
+                    out=unit_codes[:, pair, :].bitcast(FP8X4),
+                    scales=unit_scales[:, pair, :],
+                    in_=held["grouped", pair][:].rearrange("p r t -> p (r t)"),
+                )
+
+            return [add_bias_and_square, take_norm, scale_rows, flip_rows, quantise_rows]
+
+        raw_q = consts.tile([P, 2 * PAIRS * K_PASS], BF16, name="raw_q")
+        raw_q_blocks = raw_q[:].rearrange("p (s b k) -> p s b k", s=2, b=PAIRS)
+        nc.sync.dma_start(out=raw_q_blocks[:, 0], in_=query_feat.rearrange("b t m q -> m (b t) q"))
+        nc.sync.dma_start(out=raw_q_blocks[:, 1], in_=Wq.rearrange("(b p) q -> p b q", p=P))
+        raw_q_words = raw_q[:].bitcast(F32).rearrange("p (s b w) -> p s b w", s=2, b=PAIRS)
+
+        q_codes, q_scales = operand_tiles(1)
+        q_acc = accumulators()
+        spread = consts.tile([P, SPREAD], F32, name="spread")
+        qf_codes = consts.tile([P, PAIRS, P], U32, name="qf_codes", align_bytes=64)
+        qf_scales = consts.tile([P, PAIRS, P], U8, name="qf_scales", align_bytes=64)
+        query_stages = unit_row_stages(q_acc, spread[:, POSITIONS : POSITIONS + FEATURES], qf_codes, qf_scales)
+
+        def start_queries():
+            for pair in range(PAIRS):
+                project(q_codes, q_scales, 0, pair, q_acc[pair], True, True)
+            for i in range(SPREAD // FEATURES):
+                columns = slice(i * FEATURES, (i + 1) * FEATURES)
+                bank = flip_psum.tile([P, FEATURES], F32, name="spread_bank", tag="bank")
+                nc.tensor.matmul(bank[:], lhsT=ones[:], rhs=row0[:, columns], start=True, stop=True)
+                if i % 2 == 0:
+                    nc.scalar.copy(out=spread[:, columns], in_=bank[:])
+                else:
+                    nc.vector.tensor_copy(out=spread[:, columns], in_=bank[:])
+            run_tick(query_stages, 0)
+
+        positions = spread[:, 0:POSITIONS].rearrange("p (j n c) -> p j n c", j=PAIRS, c=3)
+        inv_extent = consts.tile([P, PAIRS, 3], F32, name="inv_extent")
+        shift = consts.tile([P, PAIRS, 3], F32, name="shift")
+        kept = consts.tile([P, PAIRS], F32, name="kept")
+        log_kept = consts.tile([P, PAIRS], F32, name="log_kept")
+        log_rest = consts.tile([P, PAIRS], F32, name="log_rest")
+        keep_term = consts.tile([P, PAIRS], F32, name="keep_term")
+        offsets = consts.tile([P, PAIRS, 3, P], F32, name="offsets")
+        highest = consts.tile([P, PAIRS, P], F32, name="highest")
+        lowest = consts.tile([P, PAIRS, P], F32, name="lowest")
+        gate = consts.tile([P, PAIRS, P], F32, name="gate")
+        logits = consts.tile([P, PAIRS, 1 + P], F32, name="logits")
+
+        def box_terms_and_logs():
+            sizes = box[:, :, 3:6]
+            extent = consts.tile([P, PAIRS, 3], F32, name="extent")
+            nc.vector.scalar_tensor_tensor(out=extent[:], in0=sizes, scalar=-1.0, in1=sizes, op0=ALU.mult, op1=ALU.max)
+            nc.vector.tensor_scalar(
+                out=extent[:], in0=extent[:], scalar1=MIN_EXTENT, scalar2=0.5 * DILATION, op0=ALU.max, op1=ALU.mult
+            )
+            nc.vector.reciprocal(out=inv_extent[:], in_=extent[:])
+            nc.vector.scalar_tensor_tensor(
+                out=shift[:], in0=box[:, :, 0:3], scalar=-1.0, in1=inv_extent[:], op0=ALU.mult, op1=ALU.mult
+            )
+            nc.vector.tensor_scalar(
+                out=kept[:], in0=keep[:], scalar1=KEEP_EPS, scalar2=1.0 - KEEP_EPS, op0=ALU.max, op1=ALU.min
+            )
+            nc.scalar.activation(out=log_kept[:], in_=kept[:], func=ACT.Ln)
+            nc.scalar.activation(out=log_rest[:], in_=kept[:], func=ACT.Ln, scale=-1.0, bias=1.0)
+            warm = consts.tile([P, PAIRS], F32, name="warm")
+            nc.scalar.sqrt(out=warm[:], in_=kept[:])
+
+        def finish_keep_term():
+            nc.vector.tensor_tensor(out=keep_term[:], in0=log_kept[:], in1=log_rest[:], op=ALU.subtract)
+            nc.vector.tensor_scalar_mul(out=keep_term[:], in0=keep_term[:], scalar1=KEEP_W)
+
+        def farthest_axis(pair):
+            for c in range(3):
+                nc.vector.tensor_scalar(
+                    out=offsets[:, pair, c, :],
+                    in0=positions[:, pair, :, c],
+                    scalar1=inv_extent[:, pair, c : c + 1],
+                    scalar2=shift[:, pair, c : c + 1],
+                    op0=ALU.mult,
+                    op1=ALU.add,
+                )
+            by_gaussian = offsets[:, pair].rearrange("p c n -> p n c")
+            nc.vector.tensor_reduce(out=highest[:, pair, :], in_=by_gaussian, axis=AXIS.X, op=ALU.max)
+            nc.vector.tensor_reduce(out=lowest[:, pair, :], in_=by_gaussian, axis=AXIS.X, op=ALU.min)
+            nc.vector.scalar_tensor_tensor(
+                out=gate[:, pair, :],
+                in0=lowest[:, pair, :],
+                scalar=-1.0,
+                in1=highest[:, pair, :],
+                op0=ALU.mult,
+                op1=ALU.max,
+            )
+
+        def gate_and_presence():
+            nc.vector.tensor_scalar(
+                out=gate[:], in0=gate[:], scalar1=-GATE_TEMP, scalar2=GATE_TEMP, op0=ALU.mult, op1=ALU.add
+            )
+            nc.vector.tensor_scalar(
+                out=gate[:], in0=gate[:], scalar1=-GATE_CLIP, scalar2=GATE_CLIP, op0=ALU.max, op1=ALU.min
+            )
+            nc.vector.tensor_tensor(
+                out=gate[:], in0=gate[:], in1=presence[:].unsqueeze(2).to_broadcast([P, PAIRS, P]), op=ALU.add
+            )
+
+        def flip_to_gaussian_rows():
+            bank = flip_psum.tile([P, PAIRS, P], F32, name="gate_bank", tag="bank")
+            for pair in range(PAIRS):
+                nc.tensor.transpose(bank[:, pair, :], gate[:, pair, :], ident_f32[:])
+            nc.vector.tensor_tensor(
+                out=logits[:, :, 1:], in0=bank[:], in1=keep_term[:].unsqueeze(2).to_broadcast([P, PAIRS, P]), op=ALU.add
+            )
+            nc.vector.tensor_copy(out=logits[:, :, 0:1], in_=background[:].unsqueeze(1).to_broadcast([P, PAIRS, 1]))
+
+        side_steps = [start_queries]
+        side_steps.extend([lambda tick=tick: run_tick(query_stages, tick) for tick in range(1, ticks(query_stages))])
+        side_steps.extend([box_terms_and_logs, finish_keep_term])
+        side_steps.extend([lambda pair=pair: farthest_axis(pair) for pair in range(PAIRS)])
+        side_steps.extend([gate_and_presence, flip_to_gaussian_rows])
+
+        data_rows = [
+            instance_affinity.rearrange("b t n a -> n (b t) a"),
+            motion_code.rearrange("b t n c -> n (b t) c"),
+        ]
+        weight_rows = Wg.rearrange("(b p) k -> p b k", p=P)
+
+        q_banks = flip_round([raw_q_words[:, s, 2 * half : 2 * half + 2, :] for s in range(2) for half in range(2)])
+        waiting = (
+            empty_round(q_banks),
+            [q_codes[:, 0, s, 2 * half * P : (2 * half + 2) * P] for s in range(2) for half in range(2)],
+            [q_scales[:, 0, s, 2 * half * P : (2 * half + 2) * P] for s in range(2) for half in range(2)],
+        )
+
+        g_acc = None
+        ready = None
+        for chunk in range(CHUNKS):
+            codes, scales = operand_tiles(CHUNK_PASSES)
+            for piece in range(2 * 2):
+                s, half = divmod(piece, 2)
+                blocks = slice(2 * half, 2 * half + 2)
+                first_k = chunk * CHUNK
+                raw = raws.tile([P, 2 * CHUNK], BF16, name="raw", tag="raw")
+                if s == 1:
+                    source = weight_rows[:, blocks, first_k : first_k + CHUNK]
+                elif first_k < AFFINITY:
+                    source = data_rows[0][:, blocks, first_k : first_k + CHUNK]
+                else:
+                    source = data_rows[1][:, blocks, first_k - AFFINITY : first_k - AFFINITY + CHUNK]
+                nc.sync.dma_start(out=raw[:].rearrange("p (b k) -> p b k", b=2), in_=source)
+                raw_words = raw[:].bitcast(F32).rearrange("p (b g w) -> p b g w", b=2, g=CHUNK_PASSES)
+
+                banks = flip_round([raw_words[:, :, g, :] for g in range(CHUNK_PASSES)])
+                quantise_round(*waiting)
+                columns = slice(2 * half * P, (2 * half + 2) * P)
+                waiting = (
+                    empty_round(banks),
+                    [codes[:, g, s, columns] for g in range(CHUNK_PASSES)],
+                    [scales[:, g, s, columns] for g in range(CHUNK_PASSES)],
+                )
+
+                if chunk > 0:
+                    if chunk == 1 and piece == 0:
+                        g_acc = accumulators()
+                    for pair in range(PAIRS):
+                        project(ready[0], ready[1], piece, pair, g_acc[pair], chunk == 1 and piece == 0, False)
+
+                step = chunk * 2 * 2 + piece
+                if step < len(side_steps):
+                    side_steps[step]()
+            ready = (codes, scales)
+
+        quantise_round(*waiting)
+        for pair in range(PAIRS):
+            for k_pass in range(CHUNK_PASSES):
+                project(ready[0], ready[1], k_pass, pair, g_acc[pair], False, k_pass == CHUNK_PASSES - 1)
+
+        gf_codes = consts.tile([P, PAIRS, P], U32, name="gf_codes", align_bytes=64)
+        gf_scales = consts.tile([P, PAIRS, P], U8, name="gf_scales", align_bytes=64)
+        out_rows = out.rearrange("b (t n) c -> (b t) n c", n=P)
+        held = {}
+
+        def add_similarity(pair):
+            similarity = flip_psum.tile([P, P], F32, name="similarity", tag="bank")
+            nc.tensor.matmul_mx(
+                out=similarity[:],
+                lhsT=gf_codes[:, pair, :].bitcast(FP8X4),
+                lhsT_scale=gf_scales[:, pair, :],
+                rhs=qf_codes[:, pair, :].bitcast(FP8X4),
+                rhs_scale=qf_scales[:, pair, :],
+                start=True,
+                stop=True,
+            )
+            nc.vector.scalar_tensor_tensor(
+                out=logits[:, pair, 1:],
+                in0=similarity[:],
+                scalar=FEAT_TEMP,
+                in1=logits[:, pair, 1:],
+                op0=ALU.mult,
+                op1=ALU.add,
+            )
+            top = per_pair.tile([P, 1], F32, name="top", tag="top")
+            nc.vector.reduce_max(out=top[:], in_=logits[:, pair, :], axis=AXIS.X)
+            minus_top = per_pair.tile([P, 1], F32, name="minus_top", tag="minus_top")
+            nc.vector.tensor_scalar_mul(out=minus_top[:], in0=top[:], scalar1=-1.0)
+            held["minus_top", pair] = minus_top
+
+        def exponentials(pair):
+            raised = per_pair.tile([P, 1 + P], F32, name="raised", tag="raised")
+            total = per_pair.tile([P, 1], F32, name="total", tag="total")
+            nc.scalar.activation(
+                out=raised[:], in_=logits[:, pair, :], func=ACT.Exp, bias=held["minus_top", pair][:, 0:1], accum_out=total[:]
+            )
+            held["raised", pair] = raised
+            held["total", pair] = total
+
+        def divide_and_store(pair):
+            inv_total = per_pair.tile([P, 1], F32, name="inv_total", tag="inv_total")
+            nc.vector.reciprocal(out=inv_total[:], in_=held["total", pair][:])
+            probs = per_pair.tile([P, 1 + P], F32, name="probs", tag="probs")
+            nc.vector.tensor_scalar_mul(out=probs[:], in0=held["raised", pair][:], scalar1=inv_total[:, 0:1])
+            nc.sync.dma_start(out=out_rows[pair], in_=probs[:])
+
+        final_stages = unit_row_stages(g_acc, spread[:, POSITIONS + FEATURES : SPREAD], gf_codes, gf_scales)
+        final_stages.extend([add_similarity, exponentials, divide_and_store])
+        for tick in range(ticks(final_stages)):
+            run_tick(final_stages, tick)

@@ -24,6 +24,7 @@ CHUNK_PASSES = 4
 CHUNK = CHUNK_PASSES * K_PASS
 CHUNKS = (AFFINITY + MOTION) // CHUNK
 ROUND_BANKS = 4
+RUN_BANKS = 2
 SCALAR_BANKS = 3
 BANK_VALUES = 2 * P * PACK
 RAW_BUFS = 8
@@ -94,17 +95,14 @@ def tile_gaussianqueryassignment_k_kernel(
         background = consts.tile([P, 1], BF16, name="background")
         nc.gpsimd.dma_start(out=background[:], in_=background_bias.partition_broadcast(P))
 
-        def flip_round(sources):
-            banks = []
-            for source in sources:
-                bank = flip_psum.tile([P, 2, 2, P], F32, name="bank", tag="bank")
-                for block in range(2):
-                    for half in range(2):
-                        nc.tensor.transpose(
-                            bank[:, block, half, :], source[:, block, half * P : (half + 1) * P], ident_f32[:]
-                        )
-                banks.append(bank)
-            return banks
+        def flip_bank(source):
+            bank = flip_psum.tile([P, 2, 2, P], F32, name="bank", tag="bank")
+            for block in range(2):
+                for half in range(2):
+                    nc.tensor.transpose(
+                        bank[:, block, half, :], source[:, block, half * P : (half + 1) * P], ident_f32[:]
+                    )
+            return bank
 
         def empty_round(banks):
             grouped = groupeds.tile([P, ROUND_BANKS * BANK_VALUES], BF16, name="grouped", tag="grouped", align_bytes=64)
@@ -313,21 +311,24 @@ def tile_gaussianqueryassignment_k_kernel(
         ]
         weight_rows = Wg.rearrange("(b p) k -> p b k", p=P)
 
-        q_banks = flip_round([raw_q_words[:, s, 2 * half : 2 * half + 2, :] for s in range(2) for half in range(2)])
+        q_banks = [flip_bank(raw_q_words[:, s, 2 * half : 2 * half + 2, :]) for s in range(2) for half in range(2)]
         waiting = (
             empty_round(q_banks),
             [q_codes[:, 0, s, 2 * half * P : (2 * half + 2) * P] for s in range(2) for half in range(2)],
             [q_scales[:, 0, s, 2 * half * P : (2 * half + 2) * P] for s in range(2) for half in range(2)],
         )
 
+        chunk_passes = [
+            (k_pass, pair) for half in range(2) for k_pass in range(CHUNK_PASSES) for pair in (2 * half, 2 * half + 1)
+        ]
         g_acc = None
         ready = None
         for chunk in range(CHUNKS):
             codes, scales = operand_tiles(CHUNK_PASSES)
+            first_k = chunk * CHUNK
             for piece in range(2 * 2):
-                s, half = divmod(piece, 2)
+                s, half = 1 - piece // 2, piece % 2
                 blocks = slice(2 * half, 2 * half + 2)
-                first_k = chunk * CHUNK
                 raw = raws.tile([P, 2 * CHUNK], BF16, name="raw", tag="raw")
                 if s == 1:
                     source = weight_rows[:, blocks, first_k : first_k + CHUNK]
@@ -338,20 +339,22 @@ def tile_gaussianqueryassignment_k_kernel(
                 nc.sync.dma_start(out=raw[:].rearrange("p (b k) -> p b k", b=2), in_=source)
                 raw_words = raw[:].bitcast(F32).rearrange("p (b g w) -> p b g w", b=2, g=CHUNK_PASSES)
 
-                banks = flip_round([raw_words[:, :, g, :] for g in range(CHUNK_PASSES)])
                 quantise_round(*waiting)
+                if chunk == 1 and piece == 0:
+                    g_acc = accumulators()
+                banks = []
+                for g in range(CHUNK_PASSES):
+                    banks.append(flip_bank(raw_words[:, :, g, :]))
+                    done = piece * ROUND_BANKS + g + 1
+                    if chunk > 0 and done % RUN_BANKS == 0:
+                        for k_pass, pair in chunk_passes[done - RUN_BANKS : done]:
+                            project(ready[0], ready[1], k_pass, pair, g_acc[pair], chunk == 1 and k_pass == 0, False)
                 columns = slice(2 * half * P, (2 * half + 2) * P)
                 waiting = (
                     empty_round(banks),
                     [codes[:, g, s, columns] for g in range(CHUNK_PASSES)],
                     [scales[:, g, s, columns] for g in range(CHUNK_PASSES)],
                 )
-
-                if chunk > 0:
-                    if chunk == 1 and piece == 0:
-                        g_acc = accumulators()
-                    for pair in range(PAIRS):
-                        project(ready[0], ready[1], piece, pair, g_acc[pair], chunk == 1 and piece == 0, False)
 
                 step = chunk * 2 * 2 + piece
                 if step < len(side_steps):

@@ -15,7 +15,6 @@ AXIS = mybir.AxisListType
 P = 128
 PACK = 4
 K_PASS = P * PACK
-PASS_WORDS = K_PASS // 2
 PAIRS = 4
 FEATURES = 512
 AFFINITY = 12288
@@ -23,10 +22,14 @@ MOTION = 4096
 CHUNK_PASSES = 4
 CHUNK = CHUNK_PASSES * K_PASS
 CHUNKS = (AFFINITY + MOTION) // CHUNK
-ROUND_BANKS = 4
+RAW = 2 * CHUNK
+BANK_ROWS = 2 * P
+CHUNK_BANKS = 16
+LATE_BANK = CHUNK_BANKS * (CHUNKS - 1) + 4
+FLIP_BANKS = 4
 RUN_BANKS = 2
-SCALAR_BANKS = 3
-BANK_VALUES = 2 * P * PACK
+QUANTISE_LAG = 3
+VECTOR_EVERY = 4
 RAW_BUFS = 8
 POSITIONS = PAIRS * P * 3
 SPREAD = POSITIONS + 2 * FEATURES
@@ -41,7 +44,6 @@ KEEP_EPS = 1e-4
 NORM_EPS = 1e-12
 
 FLOPS = 2 * PAIRS * P * FEATURES * (AFFINITY + MOTION + K_PASS) + 2 * PAIRS * P * P * FEATURES
-
 
 def tile_gaussianqueryassignment_k_kernel(
     tc,
@@ -64,11 +66,34 @@ def tile_gaussianqueryassignment_k_kernel(
         ctx.enter_context(tc.manual_schedule())
         consts = ctx.enter_context(tc.tile_pool(name="consts", bufs=1))
         raws = ctx.enter_context(tc.tile_pool(name="raws", bufs=RAW_BUFS))
-        groupeds = ctx.enter_context(tc.tile_pool(name="groupeds", bufs=3))
+        groupeds = ctx.enter_context(tc.tile_pool(name="groupeds", bufs=6))
+        weights = ctx.enter_context(tc.tile_pool(name="weights", bufs=2))
         operands = ctx.enter_context(tc.tile_pool(name="operands", bufs=2))
         per_pair = ctx.enter_context(tc.tile_pool(name="per_pair", bufs=PAIRS))
-        flip_psum = ctx.enter_context(tc.psum_pool(name="flip_psum", bufs=ROUND_BANKS))
+        flip_psum = ctx.enter_context(tc.psum_pool(name="flip_psum", bufs=FLIP_BANKS))
         acc_psum = ctx.enter_context(tc.psum_pool(name="acc_psum", bufs=1))
+
+        data_rows = [
+            instance_affinity.rearrange("b t n a -> n (b t) a"),
+            motion_code.rearrange("b t n c -> n (b t) c"),
+        ]
+        weight_rows = Wg.rearrange("(b p) k -> p b k", p=P)
+
+        def gaussian_rows(pairs, first_k, width):
+            if first_k < AFFINITY:
+                return data_rows[0][:, pairs, first_k : first_k + width]
+            return data_rows[1][:, pairs, first_k - AFFINITY : first_k - AFFINITY + width]
+
+        def load(source, blocks):
+            raw = raws.tile([P, RAW], BF16, name="raw", tag="raw")
+            nc.sync.dma_start(out=raw[:].rearrange("p (b k) -> p b k", b=blocks), in_=source)
+            return raw[:].bitcast(F32).rearrange("p (b g w) -> p b g w", b=blocks, w=K_PASS // 2)
+
+        raw_q = raws.tile([P, RAW], BF16, name="raw", tag="raw")
+        raw_q_blocks = raw_q[:].rearrange("p (s b k) -> p s b k", s=2, b=PAIRS)
+        nc.sync.dma_start(out=raw_q_blocks[:, 0], in_=query_feat.rearrange("b t m q -> m (b t) q"))
+        nc.sync.dma_start(out=raw_q_blocks[:, 1], in_=Wq.rearrange("(b p) q -> p b q", p=P))
+        raw_q_words = raw_q[:].bitcast(F32).rearrange("p (s b w) -> p s b w", s=2, b=PAIRS)
 
         ident_f32 = consts.tile([P, P], F32, name="ident_f32")
         make_identity(nc, ident_f32[:])
@@ -76,6 +101,8 @@ def tile_gaussianqueryassignment_k_kernel(
         make_identity(nc, ident_bf16[:])
         ones = consts.tile([P, P], BF16, name="ones")
         nc.vector.memset(ones[:], 1.0)
+        minus_half = consts.tile([P, 1], F32, name="minus_half")
+        nc.vector.memset(minus_half[:], -0.5)
 
         row0 = consts.tile([P, SPREAD], BF16, name="row0")
         nc.vector.memset(row0[:], 0.0)
@@ -95,87 +122,82 @@ def tile_gaussianqueryassignment_k_kernel(
         background = consts.tile([P, 1], BF16, name="background")
         nc.gpsimd.dma_start(out=background[:], in_=background_bias.partition_broadcast(P))
 
-        def flip_bank(source):
+        waiting = []
+        counts = {"banks": 0}
+
+        def quantise_oldest():
+            grouped, codes, scales = waiting[0]
+            waiting.remove(waiting[0])
+            nc.vector.quantize_mx(out=codes.bitcast(FP8X4), scales=scales, in_=grouped[:])
+
+        def flip_bank(source, codes, scales):
             bank = flip_psum.tile([P, 2, 2, P], F32, name="bank", tag="bank")
-            for block in range(2):
+            for unit in range(2):
                 for half in range(2):
-                    nc.tensor.transpose(
-                        bank[:, block, half, :], source[:, block, half * P : (half + 1) * P], ident_f32[:]
-                    )
-            return bank
+                    nc.tensor.transpose(bank[:, unit, half, :], source[:, unit, half * P : (half + 1) * P], ident_f32[:])
+            grouped = groupeds.tile([P, BANK_ROWS * PACK], BF16, name="grouped", tag="grouped", align_bytes=64)
+            words = grouped[:].bitcast(F32).rearrange("p (u r h) -> p u r h", u=2, h=2)
+            flipped = bank[:].rearrange("p u h r -> p u r h")
+            counts["banks"] += 1
+            if counts["banks"] % VECTOR_EVERY == 0:
+                nc.vector.tensor_copy(out=words, in_=flipped)
+            else:
+                nc.scalar.copy(out=words, in_=flipped)
+            waiting.append((grouped, codes, scales))
+            if len(waiting) > QUANTISE_LAG:
+                quantise_oldest()
 
-        def empty_round(banks):
-            grouped = groupeds.tile([P, ROUND_BANKS * BANK_VALUES], BF16, name="grouped", tag="grouped", align_bytes=64)
-            words = grouped[:].bitcast(F32).rearrange("p (i b r h) -> p i b r h", i=ROUND_BANKS, b=2, h=2)
-            for i, bank in enumerate(banks):
-                flipped = bank[:].rearrange("p b h r -> p b r h")
-                if i < SCALAR_BANKS:
-                    nc.scalar.copy(out=words[:, i], in_=flipped)
-                else:
-                    nc.vector.tensor_copy(out=words[:, i], in_=flipped)
-            return grouped
-
-        def quantise_round(grouped, codes_parts, scales_parts):
-            for i in range(ROUND_BANKS):
-                nc.vector.quantize_mx(
-                    out=codes_parts[i].bitcast(FP8X4),
-                    scales=scales_parts[i],
-                    in_=grouped[:, i * BANK_VALUES : (i + 1) * BANK_VALUES],
-                )
-
-        def operand_tiles(passes):
-            codes = operands.tile([P, passes, 2, PAIRS * P], U32, name="codes", tag="codes%d" % passes, align_bytes=64)
-            scales = operands.tile([P, passes, 2, PAIRS * P], U8, name="scales", tag="scales%d" % passes, align_bytes=64)
+        def operand(pool, tag, passes, width):
+            codes = pool.tile([P, passes, width], U32, name="codes", tag=tag + "_codes", align_bytes=64)
+            scales = pool.tile([P, passes, width], U8, name="scales", tag=tag + "_scales", align_bytes=64)
             return codes, scales
 
-        def project(codes, scales, k_pass, pair, acc, start, stop):
-            rows = slice(pair * P, (pair + 1) * P)
+        def side_by_side(view):
+            return view.rearrange("p g c -> p (g c)")
+
+        def multiply(acc, left, left_pass, left_columns, right, right_pass, start, stop):
             nc.tensor.matmul_mx(
                 out=acc[:],
-                lhsT=codes[:, k_pass, 0, rows].bitcast(FP8X4),
-                lhsT_scale=scales[:, k_pass, 0, rows],
-                rhs=codes[:, k_pass, 1, :].bitcast(FP8X4),
-                rhs_scale=scales[:, k_pass, 1, :],
+                lhsT=left[0][:, left_pass, left_columns].bitcast(FP8X4),
+                lhsT_scale=left[1][:, left_pass, left_columns],
+                rhs=right[0][:, right_pass, :].bitcast(FP8X4),
+                rhs_scale=right[1][:, right_pass, :],
                 start=start,
                 stop=stop,
             )
 
-        def accumulators():
-            return [acc_psum.tile([P, FEATURES], F32, name="acc%d" % pair, tag="acc%d" % pair) for pair in range(PAIRS)]
+        def run_tick(stages, pairs, tick):
+            for s in reversed(range(len(stages))):
+                if 0 <= tick - s < len(pairs):
+                    stages[s](pairs[tick - s])
 
-        def run_tick(stages, tick):
-            for s, stage in enumerate(stages):
-                pair = tick - s
-                if 0 <= pair < PAIRS:
-                    stage(pair)
+        def ticks(stages, pairs):
+            return len(pairs) + len(stages) - 1
 
-        def ticks(stages):
-            return PAIRS + len(stages) - 1
-
-        def unit_row_stages(acc, bias, unit_codes, unit_scales):
+        def unit_row_stages(take_acc, bias, unit_operand):
             held = {}
 
             def add_bias_and_square(pair):
                 biased = per_pair.tile([P, FEATURES], F32, name="biased", tag="biased")
-                nc.vector.tensor_tensor(out=biased[:], in0=acc[pair][:], in1=bias, op=ALU.add)
-                squares = per_pair.tile([P, FEATURES], F32, name="squares", tag="squares")
+                nc.vector.tensor_tensor(out=biased[:], in0=take_acc(pair)[:], in1=bias, op=ALU.add)
+                squares = consts.tile([P, FEATURES], F32, name="squares", tag="squares")
                 sum_squares = per_pair.tile([P, 1], F32, name="sum_squares", tag="sum_squares")
                 nc.scalar.activation(out=squares[:], in_=biased[:], func=ACT.Square, accum_out=sum_squares[:])
                 held["biased", pair] = biased
                 held["sum_squares", pair] = sum_squares
 
-            def take_norm(pair):
+            def invert_norm(pair):
                 floored = per_pair.tile([P, 1], F32, name="floored", tag="floored")
-                nc.vector.tensor_scalar_max(out=floored[:], in0=held["sum_squares", pair][:], scalar1=NORM_EPS * NORM_EPS)
-                norm = per_pair.tile([P, 1], F32, name="norm", tag="norm")
-                nc.scalar.sqrt(out=norm[:], in_=floored[:])
-                held["norm", pair] = norm
+                nc.gpsimd.tensor_scalar_max(out=floored[:], in0=held["sum_squares", pair][:], scalar1=NORM_EPS * NORM_EPS)
+                inv_norm = per_pair.tile([P, 1], F32, name="inv_norm", tag="inv_norm")
+                nc.gpsimd.tensor_tensor(out=inv_norm[:], in0=floored[:], in1=minus_half[:], op=ALU.pow)
+                held["inv_norm", pair] = inv_norm
 
             def scale_rows(pair):
-                inv_norm = per_pair.tile([P, 1], F32, name="inv_norm", tag="inv_norm")
-                nc.vector.reciprocal(out=inv_norm[:], in_=held["norm", pair][:])
                 unit = per_pair.tile([P, FEATURES], BF16, name="unit", tag="unit")
-                nc.vector.tensor_scalar_mul(out=unit[:], in0=held["biased", pair][:], scalar1=inv_norm[:, 0:1])
+                nc.vector.tensor_scalar_mul(
+                    out=unit[:], in0=held["biased", pair][:], scalar1=held["inv_norm", pair][:, 0:1]
+                )
                 held["unit", pair] = unit
 
             def flip_rows(pair):
@@ -188,29 +210,25 @@ def tile_gaussianqueryassignment_k_kernel(
 
             def quantise_rows(pair):
                 nc.vector.quantize_mx(
-                    out=unit_codes[:, pair, :].bitcast(FP8X4),
-                    scales=unit_scales[:, pair, :],
+                    out=unit_operand[0][:, pair, :].bitcast(FP8X4),
+                    scales=unit_operand[1][:, pair, :],
                     in_=held["grouped", pair][:].rearrange("p r t -> p (r t)"),
                 )
 
-            return [add_bias_and_square, take_norm, scale_rows, flip_rows, quantise_rows]
+            return [add_bias_and_square, invert_norm, scale_rows, flip_rows, quantise_rows]
 
-        raw_q = consts.tile([P, 2 * PAIRS * K_PASS], BF16, name="raw_q")
-        raw_q_blocks = raw_q[:].rearrange("p (s b k) -> p s b k", s=2, b=PAIRS)
-        nc.sync.dma_start(out=raw_q_blocks[:, 0], in_=query_feat.rearrange("b t m q -> m (b t) q"))
-        nc.sync.dma_start(out=raw_q_blocks[:, 1], in_=Wq.rearrange("(b p) q -> p b q", p=P))
-        raw_q_words = raw_q[:].bitcast(F32).rearrange("p (s b w) -> p s b w", s=2, b=PAIRS)
-
-        q_codes, q_scales = operand_tiles(1)
-        q_acc = accumulators()
+        q_operands = [operand(consts, "query", 1, PAIRS * P), operand(consts, "query_weight", 1, FEATURES)]
         spread = consts.tile([P, SPREAD], F32, name="spread")
-        qf_codes = consts.tile([P, PAIRS, P], U32, name="qf_codes", align_bytes=64)
-        qf_scales = consts.tile([P, PAIRS, P], U8, name="qf_scales", align_bytes=64)
-        query_stages = unit_row_stages(q_acc, spread[:, POSITIONS : POSITIONS + FEATURES], qf_codes, qf_scales)
+        qf = operand(consts, "qf", PAIRS, P)
 
-        def start_queries():
-            for pair in range(PAIRS):
-                project(q_codes, q_scales, 0, pair, q_acc[pair], True, True)
+        def project_queries(pair):
+            acc = flip_psum.tile([P, FEATURES], F32, name="query_sums", tag="bank")
+            multiply(acc, q_operands[0], 0, slice(pair * P, (pair + 1) * P), q_operands[1], 0, True, True)
+            return acc
+
+        query_stages = unit_row_stages(project_queries, spread[:, POSITIONS : POSITIONS + FEATURES], qf)
+
+        def spread_vectors():
             for i in range(SPREAD // FEATURES):
                 columns = slice(i * FEATURES, (i + 1) * FEATURES)
                 bank = flip_psum.tile([P, FEATURES], F32, name="spread_bank", tag="bank")
@@ -219,7 +237,6 @@ def tile_gaussianqueryassignment_k_kernel(
                     nc.scalar.copy(out=spread[:, columns], in_=bank[:])
                 else:
                     nc.vector.tensor_copy(out=spread[:, columns], in_=bank[:])
-            run_tick(query_stages, 0)
 
         positions = spread[:, 0:POSITIONS].rearrange("p (j n c) -> p j n c", j=PAIRS, c=3)
         inv_extent = consts.tile([P, PAIRS, 3], F32, name="inv_extent")
@@ -251,7 +268,7 @@ def tile_gaussianqueryassignment_k_kernel(
             nc.scalar.activation(out=log_kept[:], in_=kept[:], func=ACT.Ln)
             nc.scalar.activation(out=log_rest[:], in_=kept[:], func=ACT.Ln, scale=-1.0, bias=1.0)
             warm = consts.tile([P, PAIRS], F32, name="warm")
-            nc.scalar.sqrt(out=warm[:], in_=kept[:])
+            nc.scalar.activation(out=warm[:], in_=kept[:], func=ACT.Exp)
 
         def finish_keep_term():
             nc.vector.tensor_tensor(out=keep_term[:], in0=log_kept[:], in1=log_rest[:], op=ALU.subtract)
@@ -299,89 +316,23 @@ def tile_gaussianqueryassignment_k_kernel(
             )
             nc.vector.tensor_copy(out=logits[:, :, 0:1], in_=background[:].unsqueeze(1).to_broadcast([P, PAIRS, 1]))
 
-        side_steps = [start_queries]
-        side_steps.extend([lambda tick=tick: run_tick(query_stages, tick) for tick in range(1, ticks(query_stages))])
+        every_pair = tuple(range(PAIRS))
+        side_steps = [spread_vectors]
+        side_steps.extend(
+            [lambda tick=tick: run_tick(query_stages, every_pair, tick) for tick in range(ticks(query_stages, every_pair))]
+        )
         side_steps.extend([box_terms_and_logs, finish_keep_term])
         side_steps.extend([lambda pair=pair: farthest_axis(pair) for pair in range(PAIRS)])
         side_steps.extend([gate_and_presence, flip_to_gaussian_rows])
 
-        data_rows = [
-            instance_affinity.rearrange("b t n a -> n (b t) a"),
-            motion_code.rearrange("b t n c -> n (b t) c"),
-        ]
-        weight_rows = Wg.rearrange("(b p) k -> p b k", p=P)
-
-        q_banks = [flip_bank(raw_q_words[:, s, 2 * half : 2 * half + 2, :]) for s in range(2) for half in range(2)]
-        waiting = (
-            empty_round(q_banks),
-            [q_codes[:, 0, s, 2 * half * P : (2 * half + 2) * P] for s in range(2) for half in range(2)],
-            [q_scales[:, 0, s, 2 * half * P : (2 * half + 2) * P] for s in range(2) for half in range(2)],
-        )
-
-        chunk_passes = [
-            (k_pass, pair) for half in range(2) for k_pass in range(CHUNK_PASSES) for pair in (2 * half, 2 * half + 1)
-        ]
-        g_acc = None
-        ready = None
-        for chunk in range(CHUNKS):
-            codes, scales = operand_tiles(CHUNK_PASSES)
-            first_k = chunk * CHUNK
-            for piece in range(2 * 2):
-                s, half = 1 - piece // 2, piece % 2
-                blocks = slice(2 * half, 2 * half + 2)
-                raw = raws.tile([P, 2 * CHUNK], BF16, name="raw", tag="raw")
-                if s == 1:
-                    source = weight_rows[:, blocks, first_k : first_k + CHUNK]
-                elif first_k < AFFINITY:
-                    source = data_rows[0][:, blocks, first_k : first_k + CHUNK]
-                else:
-                    source = data_rows[1][:, blocks, first_k - AFFINITY : first_k - AFFINITY + CHUNK]
-                nc.sync.dma_start(out=raw[:].rearrange("p (b k) -> p b k", b=2), in_=source)
-                raw_words = raw[:].bitcast(F32).rearrange("p (b g w) -> p b g w", b=2, g=CHUNK_PASSES)
-
-                quantise_round(*waiting)
-                if chunk == 1 and piece == 0:
-                    g_acc = accumulators()
-                banks = []
-                for g in range(CHUNK_PASSES):
-                    banks.append(flip_bank(raw_words[:, :, g, :]))
-                    done = piece * ROUND_BANKS + g + 1
-                    if chunk > 0 and done % RUN_BANKS == 0:
-                        for k_pass, pair in chunk_passes[done - RUN_BANKS : done]:
-                            project(ready[0], ready[1], k_pass, pair, g_acc[pair], chunk == 1 and k_pass == 0, False)
-                columns = slice(2 * half * P, (2 * half + 2) * P)
-                waiting = (
-                    empty_round(banks),
-                    [codes[:, g, s, columns] for g in range(CHUNK_PASSES)],
-                    [scales[:, g, s, columns] for g in range(CHUNK_PASSES)],
-                )
-
-                step = chunk * 2 * 2 + piece
-                if step < len(side_steps):
-                    side_steps[step]()
-            ready = (codes, scales)
-
-        quantise_round(*waiting)
-        for pair in range(PAIRS):
-            for k_pass in range(CHUNK_PASSES):
-                project(ready[0], ready[1], k_pass, pair, g_acc[pair], False, k_pass == CHUNK_PASSES - 1)
-
-        gf_codes = consts.tile([P, PAIRS, P], U32, name="gf_codes", align_bytes=64)
-        gf_scales = consts.tile([P, PAIRS, P], U8, name="gf_scales", align_bytes=64)
+        gf = operand(consts, "gf", PAIRS, P)
         out_rows = out.rearrange("b (t n) c -> (b t) n c", n=P)
+        g_acc = {}
         held = {}
 
         def add_similarity(pair):
             similarity = flip_psum.tile([P, P], F32, name="similarity", tag="bank")
-            nc.tensor.matmul_mx(
-                out=similarity[:],
-                lhsT=gf_codes[:, pair, :].bitcast(FP8X4),
-                lhsT_scale=gf_scales[:, pair, :],
-                rhs=qf_codes[:, pair, :].bitcast(FP8X4),
-                rhs_scale=qf_scales[:, pair, :],
-                start=True,
-                stop=True,
-            )
+            multiply(similarity, gf, pair, slice(0, P), qf, pair, True, True)
             nc.vector.scalar_tensor_tensor(
                 out=logits[:, pair, 1:],
                 in0=similarity[:],
@@ -390,10 +341,8 @@ def tile_gaussianqueryassignment_k_kernel(
                 op0=ALU.mult,
                 op1=ALU.add,
             )
-            top = per_pair.tile([P, 1], F32, name="top", tag="top")
-            nc.vector.reduce_max(out=top[:], in_=logits[:, pair, :], axis=AXIS.X)
             minus_top = per_pair.tile([P, 1], F32, name="minus_top", tag="minus_top")
-            nc.vector.tensor_scalar_mul(out=minus_top[:], in0=top[:], scalar1=-1.0)
+            nc.vector.reduce_max(out=minus_top[:], in_=logits[:, pair, :], axis=AXIS.X, negate=True)
             held["minus_top", pair] = minus_top
 
         def exponentials(pair):
@@ -412,7 +361,72 @@ def tile_gaussianqueryassignment_k_kernel(
             nc.vector.tensor_scalar_mul(out=probs[:], in0=held["raised", pair][:], scalar1=inv_total[:, 0:1])
             nc.sync.dma_start(out=out_rows[pair], in_=probs[:])
 
-        final_stages = unit_row_stages(g_acc, spread[:, POSITIONS + FEATURES : SPREAD], gf_codes, gf_scales)
+        final_stages = unit_row_stages(g_acc.get, spread[:, POSITIONS + FEATURES : SPREAD], gf)
         final_stages.extend([add_similarity, exponentials, divide_and_store])
-        for tick in range(ticks(final_stages)):
-            run_tick(final_stages, tick)
+
+        for s in range(2):
+            for half in range(2):
+                columns = slice(half * BANK_ROWS, (half + 1) * BANK_ROWS)
+                flip_bank(
+                    raw_q_words[:, s, 2 * half : 2 * half + 2, :],
+                    q_operands[s][0][:, 0, columns],
+                    q_operands[s][1][:, 0, columns],
+                )
+
+        def chunk_banks(words, made, first_column):
+            columns = slice(first_column, first_column + BANK_ROWS)
+            return [(words[:, :, g, :], made[0][:, g, columns], made[1][:, g, columns]) for g in range(CHUNK_PASSES)]
+
+        def run_passes(passes):
+            for pair, data, weight, chunk, g in passes:
+                if (chunk, g) == (0, 0):
+                    g_acc[pair] = acc_psum.tile([P, FEATURES], F32, name="sums", tag="sums%d" % pair)
+                k_pass = chunk * CHUNK_PASSES + g
+                multiply(
+                    g_acc[pair],
+                    data,
+                    g,
+                    slice(pair * P, (pair + 1) * P),
+                    weight,
+                    g,
+                    k_pass == 0,
+                    k_pass == CHUNKS * CHUNK_PASSES - 1,
+                )
+
+        passes = []
+        filled, done, step = 0, 0, 0
+        for chunk in range(CHUNKS):
+            first_k = chunk * CHUNK
+            made_weights = operand(weights, "weights", CHUNK_PASSES, FEATURES)
+            made_data = operand(operands, "data", CHUNK_PASSES, PAIRS * P)
+            banks = []
+            for half in range(2):
+                blocks = slice(2 * half, 2 * half + 2)
+                banks.extend(chunk_banks(load(weight_rows[:, blocks, first_k : first_k + CHUNK], 2), made_weights, half * BANK_ROWS))
+            for half in range(2):
+                blocks = slice(2 * half, 2 * half + 2)
+                banks.extend(chunk_banks(load(gaussian_rows(blocks, first_k, CHUNK), 2), made_data, half * BANK_ROWS))
+            passes.extend(
+                [
+                    (pair, made_data, made_weights, chunk, g)
+                    for half in range(2)
+                    for pair in (2 * half, 2 * half + 1)
+                    for g in range(CHUNK_PASSES)
+                ]
+            )
+            for bank in banks:
+                flip_bank(*bank)
+                filled += 1
+                if filled % RUN_BANKS == 0:
+                    until = max(filled - CHUNK_BANKS, 0) + max(filled - LATE_BANK, 0) // 2
+                    run_passes(passes[done:until])
+                    done = until
+                if filled % 4 == 0 and step < len(side_steps):
+                    side_steps[step]()
+                    step += 1
+
+        while waiting:
+            quantise_oldest()
+        run_passes(passes[done:])
+        for tick in range(ticks(final_stages, every_pair)):
+            run_tick(final_stages, every_pair, tick)

@@ -15,18 +15,28 @@ AXIS = mybir.AxisListType
 P = 128
 PACK = 4
 K_PASS = P * PACK
+K_PASSES = 16384 // K_PASS
 PAIRS = 4
 FEATURES = 512
 AFFINITY = 12288
 MOTION = 4096
 CHUNK_PASSES = 4
 CHUNK = CHUNK_PASSES * K_PASS
-CHUNKS = (AFFINITY + MOTION) // CHUNK
+TURNED = 2048
+TURNED_PASSES = TURNED // K_PASS
+QUADRANT_K = TURNED // 4
+CHUNKS = (AFFINITY + MOTION - TURNED) // CHUNK
+SQUARE = 32
+TURN_WORDS = 512
+FIRST_BESIDE = 6
+BESIDE_EVERY = 4
 RAW = 2 * CHUNK
 BANK_ROWS = 2 * P
 CHUNK_BANKS = 16
-LATE_BANK = CHUNK_BANKS * (CHUNKS - 1) + 4
 FLIP_BANKS = 4
+LEFT_OVER = 8
+DELAY = 16
+SLACK = 8
 RUN_BANKS = 2
 QUANTISE_LAG = 3
 VECTOR_EVERY = 4
@@ -67,8 +77,9 @@ def tile_gaussianqueryassignment_k_kernel(
         consts = ctx.enter_context(tc.tile_pool(name="consts", bufs=1))
         raws = ctx.enter_context(tc.tile_pool(name="raws", bufs=RAW_BUFS))
         groupeds = ctx.enter_context(tc.tile_pool(name="groupeds", bufs=6))
-        weights = ctx.enter_context(tc.tile_pool(name="weights", bufs=2))
-        operands = ctx.enter_context(tc.tile_pool(name="operands", bufs=2))
+        weights = ctx.enter_context(tc.tile_pool(name="weights", bufs=3))
+        operands = ctx.enter_context(tc.tile_pool(name="operands", bufs=3))
+        turned_pool = ctx.enter_context(tc.tile_pool(name="turned_pool", bufs=1))
         per_pair = ctx.enter_context(tc.tile_pool(name="per_pair", bufs=PAIRS))
         flip_psum = ctx.enter_context(tc.psum_pool(name="flip_psum", bufs=FLIP_BANKS))
         acc_psum = ctx.enter_context(tc.psum_pool(name="acc_psum", bufs=1))
@@ -85,11 +96,21 @@ def tile_gaussianqueryassignment_k_kernel(
             return data_rows[1][:, pairs, first_k - AFFINITY : first_k - AFFINITY + width]
 
         def load(source, blocks):
-            raw = raws.tile([P, RAW], BF16, name="raw", tag="raw")
+            raw = raws.tile([P, RAW], BF16, name="raw", tag="raw", align_bytes=64)
             nc.sync.dma_start(out=raw[:].rearrange("p (b k) -> p b k", b=blocks), in_=source)
             return raw[:].bitcast(F32).rearrange("p (b g w) -> p b g w", b=blocks, w=K_PASS // 2)
 
-        raw_q = raws.tile([P, RAW], BF16, name="raw", tag="raw")
+        def load_quadrants(rows, first_k):
+            raw = raws.tile([P, RAW], BF16, name="raw", tag="raw", align_bytes=64)
+            for q in (0, 2, 1, 3):
+                from_k = first_k + q * QUADRANT_K
+                nc.sync.dma_start(
+                    out=raw[q * SQUARE : (q + 1) * SQUARE, :].rearrange("j (g k) -> j g k", k=QUADRANT_K),
+                    in_=rows[:, from_k : from_k + QUADRANT_K].rearrange("(g j) k -> j g k", j=SQUARE),
+                )
+            return raw[:].bitcast(F32)
+
+        raw_q = raws.tile([P, RAW], BF16, name="raw", tag="raw", align_bytes=64)
         raw_q_blocks = raw_q[:].rearrange("p (s b k) -> p s b k", s=2, b=PAIRS)
         nc.sync.dma_start(out=raw_q_blocks[:, 0], in_=query_feat.rearrange("b t m q -> m (b t) q"))
         nc.sync.dma_start(out=raw_q_blocks[:, 1], in_=Wq.rearrange("(b p) q -> p b q", p=P))
@@ -104,6 +125,10 @@ def tile_gaussianqueryassignment_k_kernel(
         minus_half = consts.tile([P, 1], F32, name="minus_half")
         nc.vector.memset(minus_half[:], -0.5)
 
+        keep = consts.tile([P, PAIRS], BF16, name="keep")
+        with nc.allow_non_contiguous_dma(reason="512 single values, one to a partition and pair"):
+            nc.scalar.dma_start(out=keep[:], in_=keep_score.rearrange("b t n -> n (b t)"))
+
         row0 = consts.tile([P, SPREAD], BF16, name="row0")
         nc.vector.memset(row0[:], 0.0)
         nc.scalar.dma_start(out=row0[0:1, 0:POSITIONS], in_=center.rearrange("(o b) t x -> o (b t x)", o=1))
@@ -112,48 +137,64 @@ def tile_gaussianqueryassignment_k_kernel(
         )
         nc.scalar.dma_start(out=row0[0:1, POSITIONS + FEATURES : SPREAD], in_=bg.rearrange("(o d) -> o d", o=1))
 
-        box = consts.tile([P, PAIRS, 7], BF16, name="box")
-        nc.gpsimd.dma_start(out=box[:], in_=query_box3d.rearrange("b t m f -> m (b t) f"))
-        keep = consts.tile([P, PAIRS], BF16, name="keep")
         presence = consts.tile([P, PAIRS], BF16, name="presence")
         with nc.allow_non_contiguous_dma(reason="512 single values, one to a partition and pair"):
-            nc.gpsimd.dma_start(out=keep[:], in_=keep_score.rearrange("b t n -> n (b t)"))
             nc.gpsimd.dma_start(out=presence[:], in_=presence_logit.rearrange("b t m -> m (b t)"))
+        box = consts.tile([P, PAIRS, 7], BF16, name="box")
+        nc.gpsimd.dma_start(out=box[:], in_=query_box3d.rearrange("b t m f -> m (b t) f"))
         background = consts.tile([P, 1], BF16, name="background")
         nc.gpsimd.dma_start(out=background[:], in_=background_bias.partition_broadcast(P))
 
+        fetched = consts.tile([P, 1], F32, name="fetched")
+        nc.scalar.activation(out=fetched[:], in_=ones[:, 0:1], func=ACT.Ln)
+        kept = consts.tile([P, PAIRS], F32, name="kept")
+        nc.vector.tensor_scalar(
+            out=kept[:], in0=keep[:], scalar1=KEEP_EPS, scalar2=1.0 - KEEP_EPS, op0=ALU.max, op1=ALU.min
+        )
+        log_kept = consts.tile([P, PAIRS], F32, name="log_kept")
+        nc.scalar.activation(out=log_kept[:], in_=kept[:], func=ACT.Ln)
+        log_rest = consts.tile([P, PAIRS], F32, name="log_rest")
+        nc.scalar.activation(out=log_rest[:], in_=kept[:], func=ACT.Ln, scale=-1.0, bias=1.0)
+        nc.scalar.activation(out=fetched[:], in_=ones[:, 0:1], func=ACT.Exp)
+
         waiting = []
-        counts = {"banks": 0}
+        counts = {"banks": 0, "made": 0, "quantised": 0, "passes": 0}
+        made_by = {}
 
         def quantise_oldest():
             grouped, codes, scales = waiting[0]
             waiting.remove(waiting[0])
-            nc.vector.quantize_mx(out=codes.bitcast(FP8X4), scales=scales, in_=grouped[:])
+            nc.vector.quantize_mx(out=codes.bitcast(FP8X4), scales=scales, in_=grouped)
+            counts["quantised"] += 1
 
-        def flip_bank(source, codes, scales):
+        def flip_bank(source, made, k_pass, first_column):
             bank = flip_psum.tile([P, 2, 2, P], F32, name="bank", tag="bank")
-            for unit in range(2):
+            for block in range(2):
                 for half in range(2):
-                    nc.tensor.transpose(bank[:, unit, half, :], source[:, unit, half * P : (half + 1) * P], ident_f32[:])
-            grouped = groupeds.tile([P, BANK_ROWS * PACK], BF16, name="grouped", tag="grouped", align_bytes=64)
-            words = grouped[:].bitcast(F32).rearrange("p (u r h) -> p u r h", u=2, h=2)
-            flipped = bank[:].rearrange("p u h r -> p u r h")
+                    nc.tensor.transpose(bank[:, block, half, :], source[:, block, half * P : (half + 1) * P], ident_f32[:])
             counts["banks"] += 1
-            if counts["banks"] % VECTOR_EVERY == 0:
-                nc.vector.tensor_copy(out=words, in_=flipped)
+            by_vector = counts["banks"] % VECTOR_EVERY == 0
+            group(bank[:].rearrange("p u h r -> p u r h"), by_vector, made, k_pass, first_column, BANK_ROWS)
+
+        def group(halves, by_vector, made, k_pass, first_column, width):
+            grouped = groupeds.tile([P, BANK_ROWS * PACK], BF16, name="grouped", tag="grouped", align_bytes=64)
+            columns = slice(first_column, first_column + width)
+            used = grouped[:, 0 : width * PACK]
+            words = used.bitcast(F32).rearrange("p (u r h) -> p u r h", r=halves.shape[2], h=2)
+            if by_vector:
+                nc.vector.tensor_copy(out=words, in_=halves)
             else:
-                nc.scalar.copy(out=words, in_=flipped)
-            waiting.append((grouped, codes, scales))
+                nc.scalar.copy(out=words, in_=halves)
+            made_by[made[2], k_pass, first_column] = counts["made"]
+            counts["made"] += 1
+            waiting.append((used, made[0][:, k_pass, columns], made[1][:, k_pass, columns]))
             if len(waiting) > QUANTISE_LAG:
                 quantise_oldest()
 
-        def operand(pool, tag, passes, width):
+        def operand(pool, tag, passes, width, name=None):
             codes = pool.tile([P, passes, width], U32, name="codes", tag=tag + "_codes", align_bytes=64)
             scales = pool.tile([P, passes, width], U8, name="scales", tag=tag + "_scales", align_bytes=64)
-            return codes, scales
-
-        def side_by_side(view):
-            return view.rearrange("p g c -> p (g c)")
+            return codes, scales, name
 
         def multiply(acc, left, left_pass, left_columns, right, right_pass, start, stop):
             nc.tensor.matmul_mx(
@@ -241,17 +282,12 @@ def tile_gaussianqueryassignment_k_kernel(
         positions = spread[:, 0:POSITIONS].rearrange("p (j n c) -> p j n c", j=PAIRS, c=3)
         inv_extent = consts.tile([P, PAIRS, 3], F32, name="inv_extent")
         shift = consts.tile([P, PAIRS, 3], F32, name="shift")
-        kept = consts.tile([P, PAIRS], F32, name="kept")
-        log_kept = consts.tile([P, PAIRS], F32, name="log_kept")
-        log_rest = consts.tile([P, PAIRS], F32, name="log_rest")
         keep_term = consts.tile([P, PAIRS], F32, name="keep_term")
-        offsets = consts.tile([P, PAIRS, 3, P], F32, name="offsets")
-        highest = consts.tile([P, PAIRS, P], F32, name="highest")
-        lowest = consts.tile([P, PAIRS, P], F32, name="lowest")
+        distance = consts.tile([P, 3, PAIRS, P], F32, name="distance")
         gate = consts.tile([P, PAIRS, P], F32, name="gate")
         logits = consts.tile([P, PAIRS, 1 + P], F32, name="logits")
 
-        def box_terms_and_logs():
+        def box_terms():
             sizes = box[:, :, 3:6]
             extent = consts.tile([P, PAIRS, 3], F32, name="extent")
             nc.vector.scalar_tensor_tensor(out=extent[:], in0=sizes, scalar=-1.0, in1=sizes, op0=ALU.mult, op1=ALU.max)
@@ -262,39 +298,24 @@ def tile_gaussianqueryassignment_k_kernel(
             nc.vector.scalar_tensor_tensor(
                 out=shift[:], in0=box[:, :, 0:3], scalar=-1.0, in1=inv_extent[:], op0=ALU.mult, op1=ALU.mult
             )
-            nc.vector.tensor_scalar(
-                out=kept[:], in0=keep[:], scalar1=KEEP_EPS, scalar2=1.0 - KEEP_EPS, op0=ALU.max, op1=ALU.min
-            )
-            nc.scalar.activation(out=log_kept[:], in_=kept[:], func=ACT.Ln)
-            nc.scalar.activation(out=log_rest[:], in_=kept[:], func=ACT.Ln, scale=-1.0, bias=1.0)
-            warm = consts.tile([P, PAIRS], F32, name="warm")
-            nc.scalar.activation(out=warm[:], in_=kept[:], func=ACT.Exp)
 
         def finish_keep_term():
             nc.vector.tensor_tensor(out=keep_term[:], in0=log_kept[:], in1=log_rest[:], op=ALU.subtract)
             nc.vector.tensor_scalar_mul(out=keep_term[:], in0=keep_term[:], scalar1=KEEP_W)
 
-        def farthest_axis(pair):
+        def axis_distances(pair):
             for c in range(3):
-                nc.vector.tensor_scalar(
-                    out=offsets[:, pair, c, :],
-                    in0=positions[:, pair, :, c],
-                    scalar1=inv_extent[:, pair, c : c + 1],
-                    scalar2=shift[:, pair, c : c + 1],
-                    op0=ALU.mult,
-                    op1=ALU.add,
+                nc.scalar.activation(
+                    out=distance[:, c, pair, :],
+                    in_=positions[:, pair, :, c],
+                    func=ACT.Abs,
+                    scale=inv_extent[:, pair, c : c + 1],
+                    bias=shift[:, pair, c : c + 1],
                 )
-            by_gaussian = offsets[:, pair].rearrange("p c n -> p n c")
-            nc.vector.tensor_reduce(out=highest[:, pair, :], in_=by_gaussian, axis=AXIS.X, op=ALU.max)
-            nc.vector.tensor_reduce(out=lowest[:, pair, :], in_=by_gaussian, axis=AXIS.X, op=ALU.min)
-            nc.vector.scalar_tensor_tensor(
-                out=gate[:, pair, :],
-                in0=lowest[:, pair, :],
-                scalar=-1.0,
-                in1=highest[:, pair, :],
-                op0=ALU.mult,
-                op1=ALU.max,
-            )
+
+        def farthest_axis():
+            nc.vector.tensor_tensor(out=gate[:], in0=distance[:, 0], in1=distance[:, 1], op=ALU.max)
+            nc.vector.tensor_tensor(out=gate[:], in0=gate[:], in1=distance[:, 2], op=ALU.max)
 
         def gate_and_presence():
             nc.vector.tensor_scalar(
@@ -306,6 +327,9 @@ def tile_gaussianqueryassignment_k_kernel(
             nc.vector.tensor_tensor(
                 out=gate[:], in0=gate[:], in1=presence[:].unsqueeze(2).to_broadcast([P, PAIRS, P]), op=ALU.add
             )
+
+        def nothing():
+            pass
 
         def flip_to_gaussian_rows():
             bank = flip_psum.tile([P, PAIRS, P], F32, name="gate_bank", tag="bank")
@@ -321,9 +345,9 @@ def tile_gaussianqueryassignment_k_kernel(
         side_steps.extend(
             [lambda tick=tick: run_tick(query_stages, every_pair, tick) for tick in range(ticks(query_stages, every_pair))]
         )
-        side_steps.extend([box_terms_and_logs, finish_keep_term])
-        side_steps.extend([lambda pair=pair: farthest_axis(pair) for pair in range(PAIRS)])
-        side_steps.extend([gate_and_presence, flip_to_gaussian_rows])
+        side_steps.extend([box_terms, finish_keep_term])
+        side_steps.extend([lambda pair=pair: axis_distances(pair) for pair in range(PAIRS)])
+        side_steps.extend([farthest_axis, gate_and_presence, nothing, flip_to_gaussian_rows])
 
         gf = operand(consts, "gf", PAIRS, P)
         out_rows = out.rearrange("b (t n) c -> (b t) n c", n=P)
@@ -366,67 +390,114 @@ def tile_gaussianqueryassignment_k_kernel(
 
         for s in range(2):
             for half in range(2):
-                columns = slice(half * BANK_ROWS, (half + 1) * BANK_ROWS)
-                flip_bank(
-                    raw_q_words[:, s, 2 * half : 2 * half + 2, :],
-                    q_operands[s][0][:, 0, columns],
-                    q_operands[s][1][:, 0, columns],
-                )
+                flip_bank(raw_q_words[:, s, 2 * half : 2 * half + 2, :], q_operands[s], 0, half * BANK_ROWS)
 
         def chunk_banks(words, made, first_column):
-            columns = slice(first_column, first_column + BANK_ROWS)
-            return [(words[:, :, g, :], made[0][:, g, columns], made[1][:, g, columns]) for g in range(CHUNK_PASSES)]
+            return [(words[:, :, g, :], made, g, first_column) for g in range(CHUNK_PASSES)]
 
-        def run_passes(passes):
-            for pair, data, weight, chunk, g in passes:
-                if (chunk, g) == (0, 0):
-                    g_acc[pair] = acc_psum.tile([P, FEATURES], F32, name="sums", tag="sums%d" % pair)
-                k_pass = chunk * CHUNK_PASSES + g
-                multiply(
-                    g_acc[pair],
-                    data,
-                    g,
-                    slice(pair * P, (pair + 1) * P),
-                    weight,
-                    g,
-                    k_pass == 0,
-                    k_pass == CHUNKS * CHUNK_PASSES - 1,
-                )
+        pending = []
+        pass_counts = {pair: 0 for pair in range(PAIRS)}
 
-        passes = []
-        filled, done, step = 0, 0, 0
+        def add_passes(data, weight, k_passes, half):
+            for g in range(k_passes):
+                for pair in (2 * half, 2 * half + 1):
+                    pending.append((counts["passes"], pair, data, weight, g))
+                    counts["passes"] += 1
+
+        def is_ready(number, pair, data, weight, g):
+            width = turn_rows if data is turned_data else BANK_ROWS
+            needs = [(data[2], g, pair * P // width * width)] + [(weight[2], g, column) for column in range(0, FEATURES, width)]
+            return all(need in made_by and made_by[need] < counts["quantised"] - SLACK for need in needs)
+
+        def run_pass(entry):
+            number, pair, data, weight, g = entry
+            if pass_counts[pair] == 0:
+                g_acc[pair] = acc_psum.tile([P, FEATURES], F32, name="sums", tag="sums%d" % pair)
+            pass_counts[pair] += 1
+            first, last = pass_counts[pair] == 1, pass_counts[pair] == K_PASSES
+            multiply(g_acc[pair], data, g, slice(pair * P, (pair + 1) * P), weight, g, first, last)
+            pending.remove(entry)
+
+        turned_weights = operand(turned_pool, "weights", TURNED_PASSES, FEATURES, "turned_weights")
+        turned_data = operand(turned_pool, "data", TURNED_PASSES, PAIRS * P, "turned_data")
+        turn_rows = RAW // QUADRANT_K * SQUARE
+        motion_rows = motion_code.rearrange("b t n c -> (b t n) c")
+        to_turn = [
+            (rows[first : first + turn_rows, :], first_k - TURNED, made, first)
+            for rows, first_k, made in ((Wg, AFFINITY + MOTION, turned_weights), (motion_rows, MOTION, turned_data))
+            for first in range(0, FEATURES, turn_rows)
+        ]
+
+        def turn_steps(rows, first_k, made, first_column):
+            words = load_quadrants(rows, first_k)
+            turned = turned_pool.tile([P, RAW // 2], F32, name="turned", tag="turned", align_bytes=64)
+            by_pass = turned[:].rearrange("p (n g h b j) -> p g b n j h", g=QUADRANT_K // K_PASS, h=2, b=4, j=SQUARE)
+
+            def turn(first):
+                nc.vector.transpose(out=turned[:, first : first + TURN_WORDS], in_=words[:, first : first + TURN_WORDS])
+
+            def take_pass(k_pass):
+                group(by_pass[:, k_pass // 4, k_pass % 4], False, made, k_pass, first_column, turn_rows)
+
+            return [lambda first=first: turn(first) for first in range(0, RAW // 2, TURN_WORDS)] + [
+                lambda k_pass=k_pass: take_pass(k_pass) for k_pass in range(TURNED_PASSES)
+            ]
+
+        filled, step = 0, 0
+        order = [("weights", 0, 0), ("weights", 0, 1)]
         for chunk in range(CHUNKS):
+            for half in range(2):
+                order.append(("data", chunk, half))
+                if chunk + 1 < CHUNKS:
+                    order.append(("weights", chunk + 1, half))
+        made = {}
+        steps_taken = 0
+        extra = []
+        for number, (kind, chunk, half) in enumerate(order):
             first_k = chunk * CHUNK
-            made_weights = operand(weights, "weights", CHUNK_PASSES, FEATURES)
-            made_data = operand(operands, "data", CHUNK_PASSES, PAIRS * P)
-            banks = []
-            for half in range(2):
-                blocks = slice(2 * half, 2 * half + 2)
-                banks.extend(chunk_banks(load(weight_rows[:, blocks, first_k : first_k + CHUNK], 2), made_weights, half * BANK_ROWS))
-            for half in range(2):
-                blocks = slice(2 * half, 2 * half + 2)
-                banks.extend(chunk_banks(load(gaussian_rows(blocks, first_k, CHUNK), 2), made_data, half * BANK_ROWS))
-            passes.extend(
-                [
-                    (pair, made_data, made_weights, chunk, g)
-                    for half in range(2)
-                    for pair in (2 * half, 2 * half + 1)
-                    for g in range(CHUNK_PASSES)
-                ]
-            )
-            for bank in banks:
+            if half == 0:
+                made[kind, chunk] = operand(
+                    weights if kind == "weights" else operands, kind, CHUNK_PASSES, FEATURES, "%s %d" % (kind, chunk)
+                )
+            blocks = slice(2 * half, 2 * half + 2)
+            if kind == "weights":
+                source = weight_rows[:, blocks, first_k : first_k + CHUNK]
+            else:
+                source = gaussian_rows(blocks, first_k, CHUNK)
+            banks = chunk_banks(load(source, 2), made[kind, chunk], half * BANK_ROWS)
+            if kind == "data":
+                add_passes(made[kind, chunk], made["weights", chunk], CHUNK_PASSES, half)
+            next_turn = (number - FIRST_BESIDE + 1) // BESIDE_EVERY
+            if (number - FIRST_BESIDE + 1) % BESIDE_EVERY == 0 and 0 <= next_turn < len(to_turn):
+                extra.extend(turn_steps(*to_turn[next_turn]))
+                if next_turn == len(to_turn) - 1:
+                    for turned_half in range(2):
+                        add_passes(turned_data, turned_weights, TURNED_PASSES, turned_half)
+            for place, bank in enumerate(banks):
                 flip_bank(*bank)
                 filled += 1
+                if number >= FIRST_BESIDE:
+                    due = min(len(extra), ((number - FIRST_BESIDE) * 4 + place + 1) * (RAW // 2 // TURN_WORDS + TURNED_PASSES) // (4 * BESIDE_EVERY))
+                    while steps_taken < due:
+                        extra[steps_taken]()
+                        steps_taken += 1
                 if filled % RUN_BANKS == 0:
-                    until = max(filled - CHUNK_BANKS, 0) + max(filled - LATE_BANK, 0) // 2
-                    run_passes(passes[done:until])
-                    done = until
+                    runs_left = (CHUNKS * CHUNK_BANKS - filled) // RUN_BANKS + 1
+                    passes_left = PAIRS * K_PASSES - LEFT_OVER - sum(pass_counts.values())
+                    quota = -(-passes_left // runs_left)
+                    if filled <= DELAY:
+                        quota = 0
+                    for entry in list(pending):
+                        if quota > 0 and is_ready(*entry):
+                            run_pass(entry)
+                            quota -= 1
                 if filled % 4 == 0 and step < len(side_steps):
                     side_steps[step]()
                     step += 1
 
         while waiting:
             quantise_oldest()
-        run_passes(passes[done:])
+        for entry in sorted(pending, key=lambda entry: entry[1]):
+            run_pass(entry)
         for tick in range(ticks(final_stages, every_pair)):
             run_tick(final_stages, every_pair, tick)

@@ -22,21 +22,14 @@ AFFINITY = 12288
 MOTION = 4096
 CHUNK_PASSES = 4
 CHUNK = CHUNK_PASSES * K_PASS
-TURNED = 2048
-TURNED_PASSES = TURNED // K_PASS
-QUADRANT_K = TURNED // 4
-CHUNKS = (AFFINITY + MOTION - TURNED) // CHUNK
-SQUARE = 32
-TURN_WORDS = 512
-FIRST_BESIDE = 6
-BESIDE_EVERY = 4
+CHUNKS = (AFFINITY + MOTION) // CHUNK
 RAW = 2 * CHUNK
 BANK_ROWS = 2 * P
 CHUNK_BANKS = 16
 FLIP_BANKS = 4
-LEFT_OVER = 8
+RESERVE = 8
 DELAY = 16
-SLACK = 8
+SLACK = 5
 RUN_BANKS = 2
 QUANTISE_LAG = 3
 VECTOR_EVERY = 4
@@ -79,7 +72,6 @@ def tile_gaussianqueryassignment_k_kernel(
         groupeds = ctx.enter_context(tc.tile_pool(name="groupeds", bufs=6))
         weights = ctx.enter_context(tc.tile_pool(name="weights", bufs=3))
         operands = ctx.enter_context(tc.tile_pool(name="operands", bufs=3))
-        turned_pool = ctx.enter_context(tc.tile_pool(name="turned_pool", bufs=1))
         per_pair = ctx.enter_context(tc.tile_pool(name="per_pair", bufs=PAIRS))
         flip_psum = ctx.enter_context(tc.psum_pool(name="flip_psum", bufs=FLIP_BANKS))
         acc_psum = ctx.enter_context(tc.psum_pool(name="acc_psum", bufs=1))
@@ -96,21 +88,11 @@ def tile_gaussianqueryassignment_k_kernel(
             return data_rows[1][:, pairs, first_k - AFFINITY : first_k - AFFINITY + width]
 
         def load(source, blocks):
-            raw = raws.tile([P, RAW], BF16, name="raw", tag="raw", align_bytes=64)
+            raw = raws.tile([P, RAW], BF16, name="raw", tag="raw")
             nc.sync.dma_start(out=raw[:].rearrange("p (b k) -> p b k", b=blocks), in_=source)
             return raw[:].bitcast(F32).rearrange("p (b g w) -> p b g w", b=blocks, w=K_PASS // 2)
 
-        def load_quadrants(rows, first_k):
-            raw = raws.tile([P, RAW], BF16, name="raw", tag="raw", align_bytes=64)
-            for q in (0, 2, 1, 3):
-                from_k = first_k + q * QUADRANT_K
-                nc.sync.dma_start(
-                    out=raw[q * SQUARE : (q + 1) * SQUARE, :].rearrange("j (g k) -> j g k", k=QUADRANT_K),
-                    in_=rows[:, from_k : from_k + QUADRANT_K].rearrange("(g j) k -> j g k", j=SQUARE),
-                )
-            return raw[:].bitcast(F32)
-
-        raw_q = raws.tile([P, RAW], BF16, name="raw", tag="raw", align_bytes=64)
+        raw_q = raws.tile([P, RAW], BF16, name="raw", tag="raw")
         raw_q_blocks = raw_q[:].rearrange("p (s b k) -> p s b k", s=2, b=PAIRS)
         nc.sync.dma_start(out=raw_q_blocks[:, 0], in_=query_feat.rearrange("b t m q -> m (b t) q"))
         nc.sync.dma_start(out=raw_q_blocks[:, 1], in_=Wq.rearrange("(b p) q -> p b q", p=P))
@@ -405,8 +387,7 @@ def tile_gaussianqueryassignment_k_kernel(
                     counts["passes"] += 1
 
         def is_ready(number, pair, data, weight, g):
-            width = turn_rows if data is turned_data else BANK_ROWS
-            needs = [(data[2], g, pair * P // width * width)] + [(weight[2], g, column) for column in range(0, FEATURES, width)]
+            needs = [(data[2], g, pair // 2 * BANK_ROWS), (weight[2], g, 0), (weight[2], g, BANK_ROWS)]
             return all(need in made_by and made_by[need] < counts["quantised"] - SLACK for need in needs)
 
         def run_pass(entry):
@@ -418,31 +399,6 @@ def tile_gaussianqueryassignment_k_kernel(
             multiply(g_acc[pair], data, g, slice(pair * P, (pair + 1) * P), weight, g, first, last)
             pending.remove(entry)
 
-        turned_weights = operand(turned_pool, "weights", TURNED_PASSES, FEATURES, "turned_weights")
-        turned_data = operand(turned_pool, "data", TURNED_PASSES, PAIRS * P, "turned_data")
-        turn_rows = RAW // QUADRANT_K * SQUARE
-        motion_rows = motion_code.rearrange("b t n c -> (b t n) c")
-        to_turn = [
-            (rows[first : first + turn_rows, :], first_k - TURNED, made, first)
-            for rows, first_k, made in ((Wg, AFFINITY + MOTION, turned_weights), (motion_rows, MOTION, turned_data))
-            for first in range(0, FEATURES, turn_rows)
-        ]
-
-        def turn_steps(rows, first_k, made, first_column):
-            words = load_quadrants(rows, first_k)
-            turned = turned_pool.tile([P, RAW // 2], F32, name="turned", tag="turned", align_bytes=64)
-            by_pass = turned[:].rearrange("p (n g h b j) -> p g b n j h", g=QUADRANT_K // K_PASS, h=2, b=4, j=SQUARE)
-
-            def turn(first):
-                nc.vector.transpose(out=turned[:, first : first + TURN_WORDS], in_=words[:, first : first + TURN_WORDS])
-
-            def take_pass(k_pass):
-                group(by_pass[:, k_pass // 4, k_pass % 4], False, made, k_pass, first_column, turn_rows)
-
-            return [lambda first=first: turn(first) for first in range(0, RAW // 2, TURN_WORDS)] + [
-                lambda k_pass=k_pass: take_pass(k_pass) for k_pass in range(TURNED_PASSES)
-            ]
-
         filled, step = 0, 0
         order = [("weights", 0, 0), ("weights", 0, 1)]
         for chunk in range(CHUNKS):
@@ -451,9 +407,7 @@ def tile_gaussianqueryassignment_k_kernel(
                 if chunk + 1 < CHUNKS:
                     order.append(("weights", chunk + 1, half))
         made = {}
-        steps_taken = 0
-        extra = []
-        for number, (kind, chunk, half) in enumerate(order):
+        for kind, chunk, half in order:
             first_k = chunk * CHUNK
             if half == 0:
                 made[kind, chunk] = operand(
@@ -467,30 +421,14 @@ def tile_gaussianqueryassignment_k_kernel(
             banks = chunk_banks(load(source, 2), made[kind, chunk], half * BANK_ROWS)
             if kind == "data":
                 add_passes(made[kind, chunk], made["weights", chunk], CHUNK_PASSES, half)
-            next_turn = (number - FIRST_BESIDE + 1) // BESIDE_EVERY
-            if (number - FIRST_BESIDE + 1) % BESIDE_EVERY == 0 and 0 <= next_turn < len(to_turn):
-                extra.extend(turn_steps(*to_turn[next_turn]))
-                if next_turn == len(to_turn) - 1:
-                    for turned_half in range(2):
-                        add_passes(turned_data, turned_weights, TURNED_PASSES, turned_half)
-            for place, bank in enumerate(banks):
+            for bank in banks:
                 flip_bank(*bank)
                 filled += 1
-                if number >= FIRST_BESIDE:
-                    due = min(len(extra), ((number - FIRST_BESIDE) * 4 + place + 1) * (RAW // 2 // TURN_WORDS + TURNED_PASSES) // (4 * BESIDE_EVERY))
-                    while steps_taken < due:
-                        extra[steps_taken]()
-                        steps_taken += 1
                 if filled % RUN_BANKS == 0:
-                    runs_left = (CHUNKS * CHUNK_BANKS - filled) // RUN_BANKS + 1
-                    passes_left = PAIRS * K_PASSES - LEFT_OVER - sum(pass_counts.values())
-                    quota = -(-passes_left // runs_left)
-                    if filled <= DELAY:
-                        quota = 0
-                    for entry in list(pending):
-                        if quota > 0 and is_ready(*entry):
-                            run_pass(entry)
-                            quota -= 1
+                    ready = [entry for entry in pending if is_ready(*entry)]
+                    quota = RUN_BANKS + len(ready) // RESERVE if filled > DELAY else 0
+                    for entry in ready[0:quota]:
+                        run_pass(entry)
                 if filled % 4 == 0 and step < len(side_steps):
                     side_steps[step]()
                     step += 1

@@ -27,12 +27,13 @@ RAW = 2 * CHUNK
 BANK_ROWS = 2 * P
 CHUNK_BANKS = 16
 FLIP_BANKS = 4
+STEP_EVERY = 5
 RESERVE = 8
 DELAY = 16
 SLACK = 5
 RUN_BANKS = 2
 QUANTISE_LAG = 3
-VECTOR_EVERY = 4
+VECTOR_EVERY = 5
 RAW_BUFS = 8
 POSITIONS = PAIRS * P * 3
 SPREAD = POSITIONS + 2 * FEATURES
@@ -189,8 +190,8 @@ def tile_gaussianqueryassignment_k_kernel(
                 stop=stop,
             )
 
-        def run_tick(stages, pairs, tick):
-            for s in reversed(range(len(stages))):
+        def run_tick(stages, pairs, tick, newest_first):
+            for s in range(len(stages)) if newest_first else reversed(range(len(stages))):
                 if 0 <= tick - s < len(pairs):
                     stages[s](pairs[tick - s])
 
@@ -325,7 +326,7 @@ def tile_gaussianqueryassignment_k_kernel(
         every_pair = tuple(range(PAIRS))
         side_steps = [spread_vectors]
         side_steps.extend(
-            [lambda tick=tick: run_tick(query_stages, every_pair, tick) for tick in range(ticks(query_stages, every_pair))]
+            [lambda tick=tick: run_tick(query_stages, every_pair, tick, False) for tick in range(ticks(query_stages, every_pair))]
         )
         side_steps.extend([box_terms, finish_keep_term])
         side_steps.extend([lambda pair=pair: axis_distances(pair) for pair in range(PAIRS)])
@@ -429,13 +430,14 @@ def tile_gaussianqueryassignment_k_kernel(
                     quota = RUN_BANKS + len(ready) // RESERVE if filled > DELAY else 0
                     for entry in ready[0:quota]:
                         run_pass(entry)
-                if filled % 4 == 0 and step < len(side_steps):
+                if filled % STEP_EVERY == 0 and step < len(side_steps):
                     side_steps[step]()
                     step += 1
 
+        assert step == len(side_steps)
         while waiting:
             quantise_oldest()
         for entry in sorted(pending, key=lambda entry: entry[1]):
             run_pass(entry)
         for tick in range(ticks(final_stages, every_pair)):
-            run_tick(final_stages, every_pair, tick)
+            run_tick(final_stages, every_pair, tick, True)

@@ -27,6 +27,7 @@ RAW = 2 * CHUNK
 BANK_ROWS = 2 * P
 CHUNK_BANKS = 16
 FLIP_BANKS = 4
+BUSY_BEFORE = 3
 STEP_EVERY = 5
 RESERVE = 8
 DELAY = 16
@@ -105,6 +106,8 @@ def tile_gaussianqueryassignment_k_kernel(
         make_identity(nc, ident_bf16[:])
         ones = consts.tile([P, P], BF16, name="ones")
         nc.vector.memset(ones[:], 1.0)
+        filler = consts.tile([P, FEATURES], BF16, name="filler")
+        nc.vector.memset(filler[:], 1.0)
         minus_half = consts.tile([P, 1], F32, name="minus_half")
         nc.vector.memset(minus_half[:], -0.5)
 
@@ -371,6 +374,12 @@ def tile_gaussianqueryassignment_k_kernel(
         final_stages = unit_row_stages(g_acc.get, spread[:, POSITIONS + FEATURES : SPREAD], gf)
         final_stages.extend([add_similarity, exponentials, divide_and_store])
 
+        def keep_busy(count):
+            for i in range(count):
+                idle_sums = acc_psum.tile([P, FEATURES], F32, name="sums", tag="sums%d" % (PAIRS - 1))
+                nc.tensor.matmul(idle_sums[:], lhsT=ones[:], rhs=filler[:], start=True, stop=True)
+
+        keep_busy(BUSY_BEFORE)
         for s in range(2):
             for half in range(2):
                 flip_bank(raw_q_words[:, s, 2 * half : 2 * half + 2, :], q_operands[s], 0, half * BANK_ROWS)
@@ -430,6 +439,8 @@ def tile_gaussianqueryassignment_k_kernel(
                     quota = RUN_BANKS + len(ready) // RESERVE if filled > DELAY else 0
                     for entry in ready[0:quota]:
                         run_pass(entry)
+                    if not pass_counts[PAIRS - 1] and quota == 0:
+                        keep_busy(1)
                 if filled % STEP_EVERY == 0 and step < len(side_steps):
                     side_steps[step]()
                     step += 1

from contextlib import ExitStack

import concourse.mybir as mybir
from concourse.masks import make_identity

F32 = mybir.dt.float32
BF16 = mybir.dt.bfloat16
U32 = mybir.dt.uint32
U8 = mybir.dt.uint8
FP8X4 = mybir.dt.float8_e4m3fn_x4
ALU = mybir.AluOpType
ACT = mybir.ActivationFunctionType
AXIS = mybir.AxisListType

P = 128
PACK = 4
K_PASS = P * PACK
K_PASSES = 16384 // K_PASS
PAIRS = 4
FEATURES = 512
AFFINITY = 12288
MOTION = 4096
CHUNK_PASSES = 4
CHUNK = CHUNK_PASSES * K_PASS
CHUNKS = (AFFINITY + MOTION) // CHUNK
RAW = 2 * CHUNK
BANK_ROWS = 2 * P
CHUNK_BANKS = 16
FLIP_BANKS = 4
BUSY_BEFORE = 3
STEP_EVERY = 5
RESERVE = 8
DELAY = 16
SLACK = 5
RUN_BANKS = 2
QUANTISE_LAG = 3
VECTOR_EVERY = 5
RAW_BUFS = 8
POSITIONS = PAIRS * P * 3
SPREAD = POSITIONS + 2 * FEATURES

DILATION = 1.5
MIN_EXTENT = 0.5
GATE_TEMP = 3.0
GATE_CLIP = 8.0
FEAT_TEMP = 6.0
KEEP_W = 0.5
KEEP_EPS = 1e-4
NORM_EPS = 1e-12

FLOPS = 2 * PAIRS * P * FEATURES * (AFFINITY + MOTION + K_PASS) + 2 * PAIRS * P * P * FEATURES

def tile_gaussianqueryassignment_k_kernel(
    tc,
    center,
    instance_affinity,
    motion_code,
    keep_score,
    query_box3d,
    query_feat,
    presence_logit,
    Wq,
    bq,
    Wg,
    bg,
    background_bias,
    out,
):
    nc = tc.nc
    with ExitStack() as ctx:
        ctx.enter_context(tc.manual_schedule())
        consts = ctx.enter_context(tc.tile_pool(name="consts", bufs=1))
        raws = ctx.enter_context(tc.tile_pool(name="raws", bufs=RAW_BUFS))
        groupeds = ctx.enter_context(tc.tile_pool(name="groupeds", bufs=6))
        weights = ctx.enter_context(tc.tile_pool(name="weights", bufs=3))
        operands = ctx.enter_context(tc.tile_pool(name="operands", bufs=3))
        per_pair = ctx.enter_context(tc.tile_pool(name="per_pair", bufs=PAIRS))
        flip_psum = ctx.enter_context(tc.psum_pool(name="flip_psum", bufs=FLIP_BANKS))
        acc_psum = ctx.enter_context(tc.psum_pool(name="acc_psum", bufs=1))

        data_rows = [
            instance_affinity.rearrange("b t n a -> n (b t) a"),
            motion_code.rearrange("b t n c -> n (b t) c"),
        ]
        weight_rows = Wg.rearrange("(b p) k -> p b k", p=P)

        def gaussian_rows(pairs, first_k, width):
            if first_k < AFFINITY:
                return data_rows[0][:, pairs, first_k : first_k + width]
            return data_rows[1][:, pairs, first_k - AFFINITY : first_k - AFFINITY + width]

        def load(source, blocks):
            raw = raws.tile([P, RAW], BF16, name="raw", tag="raw")
            nc.sync.dma_start(out=raw[:].rearrange("p (b k) -> p b k", b=blocks), in_=source)
            return raw[:].bitcast(F32).rearrange("p (b g w) -> p b g w", b=blocks, w=K_PASS // 2)

        raw_q = raws.tile([P, RAW], BF16, name="raw", tag="raw")
        raw_q_blocks = raw_q[:].rearrange("p (s b k) -> p s b k", s=2, b=PAIRS)
        nc.sync.dma_start(out=raw_q_blocks[:, 0], in_=query_feat.rearrange("b t m q -> m (b t) q"))
        nc.sync.dma_start(out=raw_q_blocks[:, 1], in_=Wq.rearrange("(b p) q -> p b q", p=P))
        raw_q_words = raw_q[:].bitcast(F32).rearrange("p (s b w) -> p s b w", s=2, b=PAIRS)

        ident_f32 = consts.tile([P, P], F32, name="ident_f32")
        make_identity(nc, ident_f32[:])
        ident_bf16 = consts.tile([P, P], BF16, name="ident_bf16")
        make_identity(nc, ident_bf16[:])
        ones = consts.tile([P, P], BF16, name="ones")
        nc.vector.memset(ones[:], 1.0)
        filler = consts.tile([P, FEATURES], BF16, name="filler")
        nc.vector.memset(filler[:], 1.0)
        minus_half = consts.tile([P, 1], F32, name="minus_half")
        nc.vector.memset(minus_half[:], -0.5)

        keep = consts.tile([P, PAIRS], BF16, name="keep")
        with nc.allow_non_contiguous_dma(reason="512 single values, one to a partition and pair"):
            nc.scalar.dma_start(out=keep[:], in_=keep_score.rearrange("b t n -> n (b t)"))

        row0 = consts.tile([P, SPREAD], BF16, name="row0")
        nc.vector.memset(row0[:], 0.0)
        nc.scalar.dma_start(out=row0[0:1, 0:POSITIONS], in_=center.rearrange("(o b) t x -> o (b t x)", o=1))
        nc.scalar.dma_start(
            out=row0[0:1, POSITIONS : POSITIONS + FEATURES], in_=bq.rearrange("(o d) -> o d", o=1)
        )
        nc.scalar.dma_start(out=row0[0:1, POSITIONS + FEATURES : SPREAD], in_=bg.rearrange("(o d) -> o d", o=1))

        presence = consts.tile([P, PAIRS], BF16, name="presence")
        with nc.allow_non_contiguous_dma(reason="512 single values, one to a partition and pair"):
            nc.gpsimd.dma_start(out=presence[:], in_=presence_logit.rearrange("b t m -> m (b t)"))
        box = consts.tile([P, PAIRS, 7], BF16, name="box")
        nc.gpsimd.dma_start(out=box[:], in_=query_box3d.rearrange("b t m f -> m (b t) f"))
        background = consts.tile([P, 1], BF16, name="background")
        nc.gpsimd.dma_start(out=background[:], in_=background_bias.partition_broadcast(P))

        fetched = consts.tile([P, 1], F32, name="fetched")
        nc.scalar.activation(out=fetched[:], in_=ones[:, 0:1], func=ACT.Ln)
        kept = consts.tile([P, PAIRS], F32, name="kept")
        nc.vector.tensor_scalar(
            out=kept[:], in0=keep[:], scalar1=KEEP_EPS, scalar2=1.0 - KEEP_EPS, op0=ALU.max, op1=ALU.min
        )
        log_kept = consts.tile([P, PAIRS], F32, name="log_kept")
        nc.scalar.activation(out=log_kept[:], in_=kept[:], func=ACT.Ln)
        log_rest = consts.tile([P, PAIRS], F32, name="log_rest")
        nc.scalar.activation(out=log_rest[:], in_=kept[:], func=ACT.Ln, scale=-1.0, bias=1.0)
        nc.scalar.activation(out=fetched[:], in_=ones[:, 0:1], func=ACT.Exp)

        waiting = []
        counts = {"banks": 0, "made": 0, "quantised": 0, "passes": 0}
        made_by = {}

        def quantise_oldest():
            grouped, codes, scales = waiting[0]
            waiting.remove(waiting[0])
            nc.vector.quantize_mx(out=codes.bitcast(FP8X4), scales=scales, in_=grouped)
            counts["quantised"] += 1

        def flip_bank(source, made, k_pass, first_column):
            bank = flip_psum.tile([P, 2, 2, P], F32, name="bank", tag="bank")
            for block in range(2):
                for half in range(2):
                    nc.tensor.transpose(bank[:, block, half, :], source[:, block, half * P : (half + 1) * P], ident_f32[:])
            counts["banks"] += 1
            by_vector = counts["banks"] % VECTOR_EVERY == 0
            group(bank[:].rearrange("p u h r -> p u r h"), by_vector, made, k_pass, first_column, BANK_ROWS)

        def group(halves, by_vector, made, k_pass, first_column, width):
            grouped = groupeds.tile([P, BANK_ROWS * PACK], BF16, name="grouped", tag="grouped", align_bytes=64)
            columns = slice(first_column, first_column + width)
            used = grouped[:, 0 : width * PACK]
            words = used.bitcast(F32).rearrange("p (u r h) -> p u r h", r=halves.shape[2], h=2)
            if by_vector:
                nc.vector.tensor_copy(out=words, in_=halves)
            else:
                nc.scalar.copy(out=words, in_=halves)
            made_by[made[2], k_pass, first_column] = counts["made"]
            counts["made"] += 1
            waiting.append((used, made[0][:, k_pass, columns], made[1][:, k_pass, columns]))
            if len(waiting) > QUANTISE_LAG:
                quantise_oldest()

        def operand(pool, tag, passes, width, name=None):
            codes = pool.tile([P, passes, width], U32, name="codes", tag=tag + "_codes", align_bytes=64)
            scales = pool.tile([P, passes, width], U8, name="scales", tag=tag + "_scales", align_bytes=64)
            return codes, scales, name

        def multiply(acc, left, left_pass, left_columns, right, right_pass, start, stop):
            nc.tensor.matmul_mx(
                out=acc[:],
                lhsT=left[0][:, left_pass, left_columns].bitcast(FP8X4),
                lhsT_scale=left[1][:, left_pass, left_columns],
                rhs=right[0][:, right_pass, :].bitcast(FP8X4),
                rhs_scale=right[1][:, right_pass, :],
                start=start,
                stop=stop,
            )

        def run_tick(stages, pairs, tick, newest_first):
            for s in range(len(stages)) if newest_first else reversed(range(len(stages))):
                if 0 <= tick - s < len(pairs):
                    stages[s](pairs[tick - s])

        def ticks(stages, pairs):
            return len(pairs) + len(stages) - 1

        def unit_row_stages(take_acc, bias, unit_operand):
            held = {}

            def add_bias_and_square(pair):
                biased = per_pair.tile([P, FEATURES], F32, name="biased", tag="biased")
                nc.vector.tensor_tensor(out=biased[:], in0=take_acc(pair)[:], in1=bias, op=ALU.add)
                squares = consts.tile([P, FEATURES], F32, name="squares", tag="squares")
                sum_squares = per_pair.tile([P, 1], F32, name="sum_squares", tag="sum_squares")
                nc.scalar.activation(out=squares[:], in_=biased[:], func=ACT.Square, accum_out=sum_squares[:])
                held["biased", pair] = biased
                held["sum_squares", pair] = sum_squares

            def invert_norm(pair):
                floored = per_pair.tile([P, 1], F32, name="floored", tag="floored")
                nc.gpsimd.tensor_scalar_max(out=floored[:], in0=held["sum_squares", pair][:], scalar1=NORM_EPS * NORM_EPS)
                inv_norm = per_pair.tile([P, 1], F32, name="inv_norm", tag="inv_norm")
                nc.gpsimd.tensor_tensor(out=inv_norm[:], in0=floored[:], in1=minus_half[:], op=ALU.pow)
                held["inv_norm", pair] = inv_norm

            def scale_rows(pair):
                unit = per_pair.tile([P, FEATURES], BF16, name="unit", tag="unit")
                nc.vector.tensor_scalar_mul(
                    out=unit[:], in0=held["biased", pair][:], scalar1=held["inv_norm", pair][:, 0:1]
                )
                held["unit", pair] = unit

            def flip_rows(pair):
                bank = flip_psum.tile([P, PACK, P], BF16, name="unit_bank", tag="bank")
                for t in range(PACK):
                    nc.tensor.transpose(bank[:, t, :], held["unit", pair][:, t * P : (t + 1) * P], ident_bf16[:])
                grouped = per_pair.tile([P, P, PACK], BF16, name="unit_grouped", tag="unit_grouped", align_bytes=64)
                nc.scalar.copy(out=grouped[:], in_=bank[:].rearrange("p t r -> p r t"))
                held["grouped", pair] = grouped

            def quantise_rows(pair):
                nc.vector.quantize_mx(
                    out=unit_operand[0][:, pair, :].bitcast(FP8X4),
                    scales=unit_operand[1][:, pair, :],
                    in_=held["grouped", pair][:].rearrange("p r t -> p (r t)"),
                )

            return [add_bias_and_square, invert_norm, scale_rows, flip_rows, quantise_rows]

        q_operands = [operand(consts, "query", 1, PAIRS * P), operand(consts, "query_weight", 1, FEATURES)]
        spread = consts.tile([P, SPREAD], F32, name="spread")
        qf = operand(consts, "qf", PAIRS, P)

        def project_queries(pair):
            acc = flip_psum.tile([P, FEATURES], F32, name="query_sums", tag="bank")
            multiply(acc, q_operands[0], 0, slice(pair * P, (pair + 1) * P), q_operands[1], 0, True, True)
            return acc

        query_stages = unit_row_stages(project_queries, spread[:, POSITIONS : POSITIONS + FEATURES], qf)

        def spread_vectors():
            for i in range(SPREAD // FEATURES):
                columns = slice(i * FEATURES, (i + 1) * FEATURES)
                bank = flip_psum.tile([P, FEATURES], F32, name="spread_bank", tag="bank")
                nc.tensor.matmul(bank[:], lhsT=ones[:], rhs=row0[:, columns], start=True, stop=True)
                if i % 2 == 0:
                    nc.scalar.copy(out=spread[:, columns], in_=bank[:])
                else:
                    nc.vector.tensor_copy(out=spread[:, columns], in_=bank[:])

        positions = spread[:, 0:POSITIONS].rearrange("p (j n c) -> p j n c", j=PAIRS, c=3)
        inv_extent = consts.tile([P, PAIRS, 3], F32, name="inv_extent")
        shift = consts.tile([P, PAIRS, 3], F32, name="shift")
        keep_term = consts.tile([P, PAIRS], F32, name="keep_term")
        distance = consts.tile([P, 3, PAIRS, P], F32, name="distance")
        gate = consts.tile([P, PAIRS, P], F32, name="gate")
        logits = consts.tile([P, PAIRS, 1 + P], F32, name="logits")

        def box_terms():
            sizes = box[:, :, 3:6]
            extent = consts.tile([P, PAIRS, 3], F32, name="extent")
            nc.vector.scalar_tensor_tensor(out=extent[:], in0=sizes, scalar=-1.0, in1=sizes, op0=ALU.mult, op1=ALU.max)
            nc.vector.tensor_scalar(
                out=extent[:], in0=extent[:], scalar1=MIN_EXTENT, scalar2=0.5 * DILATION, op0=ALU.max, op1=ALU.mult
            )
            nc.vector.reciprocal(out=inv_extent[:], in_=extent[:])
            nc.vector.scalar_tensor_tensor(
                out=shift[:], in0=box[:, :, 0:3], scalar=-1.0, in1=inv_extent[:], op0=ALU.mult, op1=ALU.mult
            )

        def finish_keep_term():
            nc.vector.tensor_tensor(out=keep_term[:], in0=log_kept[:], in1=log_rest[:], op=ALU.subtract)
            nc.vector.tensor_scalar_mul(out=keep_term[:], in0=keep_term[:], scalar1=KEEP_W)

        def axis_distances(pair):
            for c in range(3):
                nc.scalar.activation(
                    out=distance[:, c, pair, :],
                    in_=positions[:, pair, :, c],
                    func=ACT.Abs,
                    scale=inv_extent[:, pair, c : c + 1],
                    bias=shift[:, pair, c : c + 1],
                )

        def farthest_axis():
            nc.vector.tensor_tensor(out=gate[:], in0=distance[:, 0], in1=distance[:, 1], op=ALU.max)
            nc.vector.tensor_tensor(out=gate[:], in0=gate[:], in1=distance[:, 2], op=ALU.max)

        def gate_and_presence():
            nc.vector.tensor_scalar(
                out=gate[:], in0=gate[:], scalar1=-GATE_TEMP, scalar2=GATE_TEMP, op0=ALU.mult, op1=ALU.add
            )
            nc.vector.tensor_scalar(
                out=gate[:], in0=gate[:], scalar1=-GATE_CLIP, scalar2=GATE_CLIP, op0=ALU.max, op1=ALU.min
            )
            nc.vector.tensor_tensor(
                out=gate[:], in0=gate[:], in1=presence[:].unsqueeze(2).to_broadcast([P, PAIRS, P]), op=ALU.add
            )

        def nothing():
            pass

        def flip_to_gaussian_rows():
            bank = flip_psum.tile([P, PAIRS, P], F32, name="gate_bank", tag="bank")
            for pair in range(PAIRS):
                nc.tensor.transpose(bank[:, pair, :], gate[:, pair, :], ident_f32[:])
            nc.vector.tensor_tensor(
                out=logits[:, :, 1:], in0=bank[:], in1=keep_term[:].unsqueeze(2).to_broadcast([P, PAIRS, P]), op=ALU.add
            )
            nc.vector.tensor_copy(out=logits[:, :, 0:1], in_=background[:].unsqueeze(1).to_broadcast([P, PAIRS, 1]))

        every_pair = tuple(range(PAIRS))
        side_steps = [spread_vectors]
        side_steps.extend(
            [lambda tick=tick: run_tick(query_stages, every_pair, tick, False) for tick in range(ticks(query_stages, every_pair))]
        )
        side_steps.extend([box_terms, finish_keep_term])
        side_steps.extend([lambda pair=pair: axis_distances(pair) for pair in range(PAIRS)])
        side_steps.extend([farthest_axis, gate_and_presence, nothing, flip_to_gaussian_rows])

        gf = operand(consts, "gf", PAIRS, P)
        out_rows = out.rearrange("b (t n) c -> (b t) n c", n=P)
        g_acc = {}
        held = {}

        def add_similarity(pair):
            similarity = flip_psum.tile([P, P], F32, name="similarity", tag="bank")
            multiply(similarity, gf, pair, slice(0, P), qf, pair, True, True)
            nc.vector.scalar_tensor_tensor(
                out=logits[:, pair, 1:],
                in0=similarity[:],
                scalar=FEAT_TEMP,
                in1=logits[:, pair, 1:],
                op0=ALU.mult,
                op1=ALU.add,
            )
            minus_top = per_pair.tile([P, 1], F32, name="minus_top", tag="minus_top")
            nc.vector.reduce_max(out=minus_top[:], in_=logits[:, pair, :], axis=AXIS.X, negate=True)
            held["minus_top", pair] = minus_top

        def exponentials(pair):
            raised = per_pair.tile([P, 1 + P], F32, name="raised", tag="raised")
            total = per_pair.tile([P, 1], F32, name="total", tag="total")
            nc.scalar.activation(
                out=raised[:], in_=logits[:, pair, :], func=ACT.Exp, bias=held["minus_top", pair][:, 0:1], accum_out=total[:]
            )
            held["raised", pair] = raised
            held["total", pair] = total

        def divide_and_store(pair):
            inv_total = per_pair.tile([P, 1], F32, name="inv_total", tag="inv_total")
            nc.vector.reciprocal(out=inv_total[:], in_=held["total", pair][:])
            probs = per_pair.tile([P, 1 + P], F32, name="probs", tag="probs")
            nc.vector.tensor_scalar_mul(out=probs[:], in0=held["raised", pair][:], scalar1=inv_total[:, 0:1])
            nc.sync.dma_start(out=out_rows[pair], in_=probs[:])

        final_stages = unit_row_stages(g_acc.get, spread[:, POSITIONS + FEATURES : SPREAD], gf)
        final_stages.extend([add_similarity, exponentials, divide_and_store])

        def keep_busy(count):
            for i in range(count):
                idle_sums = acc_psum.tile([P, FEATURES], F32, name="sums", tag="sums%d" % (PAIRS - 1))
                nc.tensor.matmul(idle_sums[:], lhsT=ones[:], rhs=filler[:], start=True, stop=True)

        keep_busy(BUSY_BEFORE)
        for s in range(2):
            for half in range(2):
                flip_bank(raw_q_words[:, s, 2 * half : 2 * half + 2, :], q_operands[s], 0, half * BANK_ROWS)

        def chunk_banks(words, made, first_column):
            return [(words[:, :, g, :], made, g, first_column) for g in range(CHUNK_PASSES)]

        pending = []
        pass_counts = {pair: 0 for pair in range(PAIRS)}

        def add_passes(data, weight, k_passes, half):
            for g in range(k_passes):
                for pair in (2 * half, 2 * half + 1):
                    pending.append((counts["passes"], pair, data, weight, g))
                    counts["passes"] += 1

        def is_ready(number, pair, data, weight, g):
            needs = [(data[2], g, pair // 2 * BANK_ROWS), (weight[2], g, 0), (weight[2], g, BANK_ROWS)]
            return all(need in made_by and made_by[need] < counts["quantised"] - SLACK for need in needs)

        def run_pass(entry):
            number, pair, data, weight, g = entry
            if pass_counts[pair] == 0:
                g_acc[pair] = acc_psum.tile([P, FEATURES], F32, name="sums", tag="sums%d" % pair)
            pass_counts[pair] += 1
            first, last = pass_counts[pair] == 1, pass_counts[pair] == K_PASSES
            multiply(g_acc[pair], data, g, slice(pair * P, (pair + 1) * P), weight, g, first, last)
            pending.remove(entry)

        filled, step = 0, 0
        order = [("weights", 0, 0), ("weights", 0, 1)]
        for chunk in range(CHUNKS):
            for half in range(2):
                order.append(("data", chunk, half))
                if chunk + 1 < CHUNKS:
                    order.append(("weights", chunk + 1, half))
        made = {}
        for kind, chunk, half in order:
            first_k = chunk * CHUNK
            if half == 0:
                made[kind, chunk] = operand(
                    weights if kind == "weights" else operands, kind, CHUNK_PASSES, FEATURES, "%s %d" % (kind, chunk)
                )
            blocks = slice(2 * half, 2 * half + 2)
            if kind == "weights":
                source = weight_rows[:, blocks, first_k : first_k + CHUNK]
            else:
                source = gaussian_rows(blocks, first_k, CHUNK)
            banks = chunk_banks(load(source, 2), made[kind, chunk], half * BANK_ROWS)
            if kind == "data":
                add_passes(made[kind, chunk], made["weights", chunk], CHUNK_PASSES, half)
            for bank in banks:
                flip_bank(*bank)
                filled += 1
                if filled % RUN_BANKS == 0:
                    ready = [entry for entry in pending if is_ready(*entry)]
                    quota = RUN_BANKS + len(ready) // RESERVE if filled > DELAY else 0
                    for entry in ready[0:quota]:
                        run_pass(entry)
                    if not pass_counts[PAIRS - 1] and quota == 0:
                        keep_busy(1)
                if filled % STEP_EVERY == 0 and step < len(side_steps):
                    side_steps[step]()
                    step += 1

        assert step == len(side_steps)
        while waiting:
            quantise_oldest()
        for entry in sorted(pending, key=lambda entry: entry[1]):
            run_pass(entry)
        for tick in range(ticks(final_stages, every_pair)):
            run_tick(final_stages, every_pair, tick, True)
